import numpy as np
import ml_dtypes


def mxq(x, axis, fmt="e4m3"):
    dtype, down = {"e4m3": (ml_dtypes.float8_e4m3fn, 7), "e5m2": (ml_dtypes.float8_e5m2, 14)}[fmt]
    v = np.moveaxis(np.asarray(x, np.float32).astype(ml_dtypes.bfloat16).astype(np.float64), axis, -1)
    blocks = v.reshape(v.shape[:-1] + (-1, 32))
    amax = np.abs(blocks).max(-1, keepdims=True)
    byte = np.maximum(np.where(amax > 0, np.frexp(amax)[1] - 1 + 127, 0) - down, 1)
    scale = np.exp2(byte - 127.0)
    codes = (blocks / scale).astype(np.float32).astype(dtype).astype(np.float64)
    return np.moveaxis((codes * scale).reshape(v.shape), -1, axis)


WIDE = False


def mx_kscale(k):
    if not WIDE:
        return np.ones(k)
    levels = np.array([10, -10, 5, -5, 0])
    if k % 512:
        return np.exp2(np.random.permutation(np.resize(levels, k // 32))).repeat(32)
    a = np.empty((k // 512, 16))
    for p in range(k // 512):
        a[p, :8] = np.random.permutation(np.resize(levels, 8))
        for g in range(8):
            far = levels[np.abs(levels - a[p, g]) >= 10]
            a[p, g + 8] = far[np.random.randint(len(far))]
    return np.exp2(a.ravel()).repeat(32)


BF16 = ml_dtypes.bfloat16


def bf(x):
    return np.asarray(x, np.float32).astype(BF16)


def f64(x):
    return np.asarray(x).astype(np.float64)


B, P_DIM, H_DIM, X_DIM = 512, 512, 1024, 512


def sigmoid(v):
    return 1.0 / (1.0 + np.exp(-v))


def setup_inputs():
    sp, sh, sx = mx_kscale(P_DIM), mx_kscale(H_DIM), mx_kscale(X_DIM)

    def lin_w(in_d, s):
        return bf(np.random.standard_normal((H_DIM, in_d)) * 0.6 / np.sqrt(in_d) / s[None, :])

    def lin_b():
        return bf(np.random.standard_normal(H_DIM) * 0.5)

    return {
        "P": bf(np.random.standard_normal((B, P_DIM)) * sp),
        "hidden": bf(np.random.standard_normal((B, H_DIM)) * sh),
        "cell": bf(np.random.standard_normal((B, H_DIM))),
        "ext_input": bf(np.random.standard_normal((B, X_DIM)) * sx),
        "W_pi": lin_w(P_DIM, sp), "b_pi": lin_b(),
        "W_pf": lin_w(P_DIM, sp), "b_pf": lin_b(),
        "W_pg": lin_w(P_DIM, sp), "b_pg": lin_b(),
        "W_po": lin_w(P_DIM, sp), "b_po": lin_b(),
        "W_hi": lin_w(H_DIM, sh), "W_hf": lin_w(H_DIM, sh),
        "W_hg": lin_w(H_DIM, sh), "W_ho": lin_w(H_DIM, sh),
        "W_xi": lin_w(X_DIM, sx), "W_xf": lin_w(X_DIM, sx),
        "W_xg": lin_w(X_DIM, sx), "W_xo": lin_w(X_DIM, sx),
    }


def reference(P, hidden, cell, ext_input,
              W_pi, b_pi, W_pf, b_pf, W_pg, b_pg, W_po, b_po,
              W_hi, W_hf, W_hg, W_ho,
              W_xi, W_xf, W_xg, W_xo):
    Wp = np.concatenate([f64(W_pi), f64(W_pf), f64(W_pg), f64(W_po)], axis=0)
    bp = np.concatenate([f64(b_pi), f64(b_pf), f64(b_pg), f64(b_po)], axis=0)
    Wh = np.concatenate([f64(W_hi), f64(W_hf), f64(W_hg), f64(W_ho)], axis=0)
    Wx = np.concatenate([f64(W_xi), f64(W_xf), f64(W_xg), f64(W_xo)], axis=0)
    gates = ((mxq(f64(P), 1, "e4m3") @ mxq(Wp, 1, "e4m3").T) + bp
             + (mxq(f64(hidden), 1, "e4m3") @ mxq(Wh, 1, "e4m3").T)
             + (mxq(f64(ext_input), 1, "e4m3") @ mxq(Wx, 1, "e4m3").T))
    gi, gf, gg, go = np.split(gates, 4, axis=-1)
    i = sigmoid(gi)
    f = sigmoid(gf)
    g = np.tanh(gg)
    o = sigmoid(go)
    c_new = f * f64(cell) + i * g
    h_new = o * np.tanh(c_new)
    return (h_new, c_new)

@@ -1,0 +1,341 @@
+from contextlib import ExitStack
+
+import concourse.mybir as mybir
+from concourse.masks import make_identity
+
+F32 = mybir.dt.float32
+BF16 = mybir.dt.bfloat16
+U32 = mybir.dt.uint32
+U8 = mybir.dt.uint8
+FP8X4 = mybir.dt.float8_e4m3fn_x4
+ACT = mybir.ActivationFunctionType
+ALU = mybir.AluOpType
+
+BATCH = 512
+HIDDEN = 1024
+K_TOTAL = 2048
+FLOPS = 2 * BATCH * K_TOTAL * 4 * HIDDEN
+
+P = 128
+N_TILES = BATCH // P
+N_BLOCKS = HIDDEN // P
+N_CHUNKS = 4
+N_GATES = 4
+GATE_COLS = N_GATES * P
+CHUNK_WORDS = 256
+ACTS = -1
+RAW_BLOCKS = 5
+
+
+def tile_structuredlstmcell_kernel(
+    tc, p_in, hidden, cell, ext_input,
+    W_pi, b_pi, W_pf, b_pf, W_pg, b_pg, W_po, b_po,
+    W_hi, W_hf, W_hg, W_ho,
+    W_xi, W_xf, W_xg, W_xo,
+    out_0, out_1,
+):
+    nc = tc.nc
+    weights = [
+        [W_pi, W_pf, W_po, W_pg],
+        [W_xi, W_xf, W_xo, W_xg],
+        [W_hi, W_hf, W_ho, W_hg],
+    ]
+    biases = [b_pi, b_pf, b_po, b_pg]
+    activations = [p_in, ext_input, hidden]
+    k_of = [512, 512, 1024]
+    col_i, col_f, col_o, col_g = [slice(g * P, (g + 1) * P) for g in range(N_GATES)]
+
+    with ExitStack() as ctx:
+        ctx.enter_context(tc.manual_schedule())
+        const = ctx.enter_context(tc.tile_pool(name="const", bufs=1))
+        raw_pool = ctx.enter_context(tc.tile_pool(name="raw", bufs=RAW_BLOCKS))
+        grouped_pool = ctx.enter_context(tc.tile_pool(name="grouped", bufs=6))
+        code_pool = ctx.enter_context(tc.tile_pool(name="codes", bufs=10))
+        gate_pool = ctx.enter_context(tc.tile_pool(name="gates", bufs=4))
+        out_pool = ctx.enter_context(tc.tile_pool(name="outs", bufs=3))
+        psum = ctx.enter_context(tc.psum_pool(name="psum", bufs=1))
+
+        ident_f32 = const.tile([P, P], F32, name="ident_f32")
+        make_identity(nc, ident_f32[:])
+        bias_rows = const.tile([P, GATE_COLS], BF16, name="bias_rows")
+        nc.vector.memset(bias_rows[:], 0.0)
+        warm = const.tile([P, 1], F32, name="warm")
+        nc.vector.memset(warm[:], 0.0)
+        for g in range(N_GATES):
+            nc.scalar.dma_start(
+                out=bias_rows[2 * g:2 * g + 2, :], in_=biases[g].rearrange("(r n) -> r n", r=2)
+            )
+        nc.scalar.activation(out=warm[:], in_=warm[:], func=ACT.Sigmoid)
+        ident_bf16 = const.tile([P, P], BF16, name="ident_bf16")
+        nc.vector.tensor_copy(out=ident_bf16[:], in_=ident_f32[:])
+        bias_all = const.tile([P, N_GATES, HIDDEN], BF16, name="bias_all")
+        cell_sb = const.tile([P, N_TILES, HIDDEN], BF16, name="cell_sb")
+        act_codes = const.tile([P, N_CHUNKS, BATCH], U32, name="act_codes", align_bytes=64)
+        act_scales = const.tile([P, N_CHUNKS, BATCH], U8, name="act_scales", align_bytes=64)
+
+        raw = {}
+
+        def load_activation(s):
+            raw[(ACTS, s)] = const.tile([P, N_TILES * k_of[s]], BF16, name="raw_act%d" % s)
+            view = activations[s].rearrange("(p t) k -> p (t k)", t=N_TILES)
+            half_cols = 2 * k_of[s]
+            for part in range(2):
+                cols = slice(part * half_cols, (part + 1) * half_cols)
+                nc.sync.dma_start(out=raw[(ACTS, s)][:, cols], in_=view[:, cols])
+
+        def load_weights(j, s):
+            k = k_of[s]
+            raw[(j, s)] = raw_pool.tile([P, N_GATES * k], BF16, name="raw_w%d" % s, tag="raw_w%d" % s)
+            for g in range(N_GATES):
+                nc.sync.dma_start(out=raw[(j, s)][:, g * k:(g + 1) * k], in_=weights[s][g][j * P:(j + 1) * P, :])
+
+        def load_block(j):
+            for s in range(3):
+                load_weights(j, s)
+
+        for s in range(3):
+            load_activation(s)
+            load_weights(0, s)
+        load_block(1)
+        nc.sync.dma_start(
+            out=cell_sb[:].rearrange("p t h -> p (t h)"), in_=cell.rearrange("(p t) h -> p (t h)", t=N_TILES)
+        )
+        for j in range(2, RAW_BLOCKS):
+            load_block(j)
+
+        free_banks = list(range(8))
+
+        def take_bank(shape):
+            b = free_banks.pop(0)
+            return b, psum.tile(shape, F32, name="bank%d" % b, tag="bank%d" % b)
+
+        grouped = {}
+        w_codes = {}
+        acc = {}
+        gates = {}
+        c_new = {}
+        h_new = {}
+
+        def transpose_chunk(j, c, engines):
+            s = min(c, 2)
+            first_word = CHUNK_WORDS * (c - 2) if c > 2 else 0
+            words = raw[(j, s)][:].bitcast(F32)
+            out_tile = grouped_pool.tile([P, 4 * GATE_COLS], BF16, name="grouped", tag="grouped", align_bytes=64)
+            grouped[(j, c)] = out_tile
+            out_words = out_tile[:].bitcast(F32)
+            banks = []
+            for half in range(2):
+                b, bank = take_bank([P, 2, 2 * P])
+                for rg in range(2):
+                    for u in range(2):
+                        col = (2 * half + rg) * (k_of[s] // 2) + first_word
+                        nc.tensor.transpose(
+                            bank[:, u, rg * P:(rg + 1) * P], words[:, col + u:col + CHUNK_WORDS:2], ident_f32[:]
+                        )
+                banks.append((b, bank))
+            for half in range(2):
+                b, bank = banks[half]
+                dst = out_words[:, half * GATE_COLS:(half + 1) * GATE_COLS].rearrange("p (n u) -> p n u", u=2)
+                src = bank[:].rearrange("p u n -> p n u")
+                if engines[half] == "s":
+                    nc.scalar.copy(out=dst, in_=src)
+                else:
+                    nc.vector.tensor_copy(out=dst, in_=src)
+                free_banks.append(b)
+
+        def quantise(j, c):
+            if j == ACTS:
+                codes, scales = act_codes[:, c, :], act_scales[:, c, :]
+            else:
+                codes_tile = code_pool.tile([P, GATE_COLS], U32, name="w_codes", tag="w_codes", align_bytes=64)
+                scales_tile = code_pool.tile([P, GATE_COLS], U8, name="w_scales", tag="w_scales", align_bytes=64)
+                w_codes[(j, c)] = (codes_tile, scales_tile)
+                codes, scales = codes_tile[:], scales_tile[:]
+            nc.vector.quantize_mx(out=codes.bitcast(FP8X4), scales=scales, in_=grouped[(j, c)][:])
+
+        def mx_pass(j, t, c):
+            if c == 0:
+                acc[(j, t)] = take_bank([P, GATE_COLS])
+            codes_tile, scales_tile = w_codes[(j, c)]
+            rows = slice(t * P, (t + 1) * P)
+            nc.tensor.matmul_mx(
+                out=acc[(j, t)][1][:],
+                lhsT=act_codes[:, c, rows].bitcast(FP8X4),
+                lhsT_scale=act_scales[:, c, rows],
+                rhs=codes_tile[:].bitcast(FP8X4),
+                rhs_scale=scales_tile[:],
+                start=(c == 0),
+                stop=(c == N_CHUNKS - 1),
+            )
+
+        def spread_bias(first_row):
+            for r in range(first_row, first_row + 4):
+                b, bank = take_bank([P, GATE_COLS])
+                nc.tensor.matmul(
+                    out=bank[:], lhsT=ident_bf16[:, r:r + 1].to_broadcast([P, P]), rhs=bias_rows[:], start=True, stop=True
+                )
+                dst = bias_all[:, r // 2, (r % 2) * GATE_COLS:(r % 2 + 1) * GATE_COLS]
+                if r % 2 == 0:
+                    nc.scalar.copy(out=dst, in_=bank[:])
+                else:
+                    nc.vector.tensor_copy(out=dst, in_=bank[:])
+                free_banks.append(b)
+
+        def add_bias(j, t):
+            if t == 0:
+                gates[j] = gate_pool.tile([P, N_TILES, GATE_COLS], F32, name="gates", tag="gates")
+            b, bank = acc[(j, t)]
+            nc.vector.tensor_tensor(
+                out=gates[j][:, t, :].rearrange("p (g n) -> p g n", g=N_GATES),
+                in0=bank[:].rearrange("p (g n) -> p g n", g=N_GATES),
+                in1=bias_all[:, :, j * P:(j + 1) * P],
+                op=ALU.add,
+            )
+            free_banks.append(b)
+
+        def passes_and_bias(j, t):
+            for c in range(N_CHUNKS):
+                mx_pass(j, t, c)
+            add_bias(j, t)
+
+        def sigmoids(j, t0, t1):
+            v = gates[j][:, t0:t1, 0:3 * P]
+            nc.scalar.activation(out=v, in_=v, func=ACT.Sigmoid)
+
+        def tanh_candidate(j, t0, t1):
+            v = gates[j][:, t0:t1, col_g]
+            nc.scalar.activation(out=v, in_=v, func=ACT.Tanh)
+
+        def forget_times_cell(j, t0, t1):
+            v = gates[j][:, t0:t1, col_f]
+            nc.vector.tensor_tensor(out=v, in0=v, in1=cell_sb[:, t0:t1, j * P:(j + 1) * P], op=ALU.mult)
+
+        def input_times_candidate(j, t0, t1):
+            v = gates[j][:, t0:t1, col_i]
+            nc.vector.tensor_tensor(out=v, in0=v, in1=gates[j][:, t0:t1, col_g], op=ALU.mult)
+
+        def sum_to_cell(j, t0, t1):
+            if j not in c_new:
+                c_new[j] = out_pool.tile([P, N_TILES, P], F32, name="c_new", tag="c_new")
+            nc.vector.tensor_tensor(
+                out=c_new[j][:, t0:t1, :], in0=gates[j][:, t0:t1, col_f], in1=gates[j][:, t0:t1, col_i], op=ALU.add
+            )
+
+        def tanh_cell(j, t0, t1):
+            nc.scalar.activation(out=gates[j][:, t0:t1, col_g], in_=c_new[j][:, t0:t1, :], func=ACT.Tanh)
+
+        def output_times_tanh(j, t0, t1):
+            if j not in h_new:
+                h_new[j] = out_pool.tile([P, N_TILES, P], F32, name="h_new", tag="h_new")
+            nc.vector.tensor_tensor(
+                out=h_new[j][:, t0:t1, :], in0=gates[j][:, t0:t1, col_o], in1=gates[j][:, t0:t1, col_g], op=ALU.mult
+            )
+
+        h_dram = out_0.rearrange("(p t) h -> p t h", t=N_TILES)
+        c_dram = out_1.rearrange("(p t) h -> p t h", t=N_TILES)
+
+        def store(dram, tiles, j, t0, t1):
+            nc.sync.dma_start(out=dram[:, t0:t1, j * P:(j + 1) * P], in_=tiles[j][:, t0:t1, :])
+
+        transpose_chunk(ACTS, 0, "sv")
+        spread_bias(0)
+        transpose_chunk(0, 0, "sv")
+        quantise(ACTS, 0)
+        transpose_chunk(ACTS, 1, "sv")
+        quantise(0, 0)
+        spread_bias(4)
+        transpose_chunk(0, 1, "sv")
+        quantise(ACTS, 1)
+        transpose_chunk(ACTS, 2, "ss")
+        quantise(0, 1)
+        transpose_chunk(ACTS, 3, "ss")
+        for c in (0, 1):
+            for t in range(N_TILES):
+                mx_pass(0, t, c)
+        quantise(ACTS, 2)
+        quantise(ACTS, 3)
+        transpose_chunk(0, 2, "ss")
+        transpose_chunk(0, 3, "ss")
+        load_block(RAW_BLOCKS)
+        quantise(0, 2)
+        quantise(0, 3)
+        transpose_chunk(1, 0, "ss")
+        transpose_chunk(1, 1, "ss")
+        for c in (2, 3):
+            for t in range(N_TILES):
+                mx_pass(0, t, c)
+        quantise(1, 0)
+        quantise(1, 1)
+        for t in range(N_TILES):
+            add_bias(0, t)
+        transpose_chunk(1, 2, "ss")
+        transpose_chunk(1, 3, "ss")
+        load_block(RAW_BLOCKS + 1)
+        quantise(1, 2)
+        quantise(1, 3)
+
+        for j in range(1, N_BLOCKS - 1):
+            transpose_chunk(j + 1, 0, "ss")
+            transpose_chunk(j + 1, 1, "ss")
+            quantise(j + 1, 0)
+            quantise(j + 1, 1)
+            sigmoids(j - 1, 0, N_TILES)
+            tanh_candidate(j - 1, 0, N_TILES)
+            passes_and_bias(j, 0)
+            passes_and_bias(j, 1)
+            forget_times_cell(j - 1, 0, N_TILES)
+            input_times_candidate(j - 1, 0, N_TILES)
+            sum_to_cell(j - 1, 0, N_TILES)
+            store(c_dram, c_new, j - 1, 0, N_TILES)
+            transpose_chunk(j + 1, 2, "ss")
+            transpose_chunk(j + 1, 3, "ss")
+            if j + 1 + RAW_BLOCKS < N_BLOCKS:
+                load_block(j + 1 + RAW_BLOCKS)
+            tanh_cell(j - 1, 0, N_TILES)
+            quantise(j + 1, 2)
+            quantise(j + 1, 3)
+            passes_and_bias(j, 2)
+            output_times_tanh(j - 1, 0, N_TILES)
+            store(h_dram, h_new, j - 1, 0, N_TILES)
+            passes_and_bias(j, 3)
+
+        last = N_BLOCKS - 1
+        prev = last - 1
+        sigmoids(prev, 0, 2)
+        tanh_candidate(prev, 0, 2)
+        sigmoids(prev, 2, 4)
+        tanh_candidate(prev, 2, 4)
+        forget_times_cell(prev, 0, 2)
+        passes_and_bias(last, 0)
+        input_times_candidate(prev, 0, 2)
+        passes_and_bias(last, 1)
+        sum_to_cell(prev, 0, 2)
+        forget_times_cell(prev, 2, 4)
+        sigmoids(last, 0, 2)
+        tanh_cell(prev, 0, 2)
+        tanh_candidate(last, 0, 2)
+        passes_and_bias(last, 2)
+        output_times_tanh(prev, 0, 2)
+        passes_and_bias(last, 3)
+        input_times_candidate(prev, 2, 4)
+        sum_to_cell(prev, 2, 4)
+        store(c_dram, c_new, prev, 0, N_TILES)
+        sigmoids(last, 2, 4)
+        tanh_cell(prev, 2, 4)
+        tanh_candidate(last, 2, 4)
+        forget_times_cell(last, 0, 2)
+        input_times_candidate(last, 0, 2)
+        output_times_tanh(prev, 2, 4)
+        store(h_dram, h_new, prev, 0, N_TILES)
+        sum_to_cell(last, 0, 2)
+        store(c_dram, c_new, last, 0, 2)
+        tanh_cell(last, 0, 2)
+        forget_times_cell(last, 2, 4)
+        input_times_candidate(last, 2, 4)
+        output_times_tanh(last, 0, 2)
+        store(h_dram, h_new, last, 0, 2)
+        sum_to_cell(last, 2, 4)
+        store(c_dram, c_new, last, 2, 4)
+        tanh_cell(last, 2, 4)
+        output_times_tanh(last, 2, 4)
+        store(h_dram, h_new, last, 2, 4)

@@ -24,6 +24,7 @@ N_GATES = 4
 GATE_COLS = N_GATES * P
 CHUNK_WORDS = 256
 ACTS = -1
+WARM_UP_MATMULS = 4
 RAW_BLOCKS = 5
 
 
@@ -49,6 +50,7 @@ def tile_structuredlstmcell_kernel(
         ctx.enter_context(tc.manual_schedule())
         const = ctx.enter_context(tc.tile_pool(name="const", bufs=1))
         raw_pool = ctx.enter_context(tc.tile_pool(name="raw", bufs=RAW_BLOCKS))
+        sorted_pool = ctx.enter_context(tc.tile_pool(name="sorted", bufs=4))
         grouped_pool = ctx.enter_context(tc.tile_pool(name="grouped", bufs=6))
         code_pool = ctx.enter_context(tc.tile_pool(name="codes", bufs=10))
         gate_pool = ctx.enter_context(tc.tile_pool(name="gates", bufs=4))
@@ -59,6 +61,8 @@ def tile_structuredlstmcell_kernel(
         make_identity(nc, ident_f32[:])
         bias_rows = const.tile([P, GATE_COLS], BF16, name="bias_rows")
         nc.vector.memset(bias_rows[:], 0.0)
+        zeros = const.tile([P, GATE_COLS], BF16, name="zeros")
+        nc.vector.memset(zeros[:], 0.0)
         warm = const.tile([P, 1], F32, name="warm")
         nc.vector.memset(warm[:], 0.0)
         for g in range(N_GATES):
@@ -109,6 +113,11 @@ def tile_structuredlstmcell_kernel(
             b = free_banks.pop(0)
             return b, psum.tile(shape, F32, name="bank%d" % b, tag="bank%d" % b)
 
+        b_warm, warm_bank = take_bank([P, GATE_COLS])
+        for i in range(WARM_UP_MATMULS):
+            nc.tensor.matmul(out=warm_bank[:], lhsT=zeros[:, 0:P], rhs=zeros[:], start=True, stop=True)
+        free_banks.append(b_warm)
+
         grouped = {}
         w_codes = {}
         acc = {}
@@ -116,10 +125,25 @@ def tile_structuredlstmcell_kernel(
         c_new = {}
         h_new = {}
 
-        def transpose_chunk(j, c, engines):
+        sorted_words = {}
+
+        def chunk_words(j, c):
             s = min(c, 2)
             first_word = CHUNK_WORDS * (c - 2) if c > 2 else 0
-            words = raw[(j, s)][:].bitcast(F32)
+            words = raw[(j, s)][:].bitcast(F32).rearrange("p (r w) -> p r w", r=4)
+            return words[:, :, first_word:first_word + CHUNK_WORDS]
+
+        def sort_words(j, c, engine="v"):
+            tile = sorted_pool.tile([P, 4, 2, P], F32, name="sorted_words", tag="sorted_words")
+            src = chunk_words(j, c).rearrange("p r (w u) -> p r u w", u=2)
+            if engine == "v":
+                nc.vector.tensor_copy(out=tile[:], in_=src)
+            else:
+                nc.scalar.copy(out=tile[:], in_=src)
+            sorted_words[(j, c)] = tile
+
+        def transpose_chunk(j, c, engines):
+            words = chunk_words(j, c)
             out_tile = grouped_pool.tile([P, 4 * GATE_COLS], BF16, name="grouped", tag="grouped", align_bytes=64)
             grouped[(j, c)] = out_tile
             out_words = out_tile[:].bitcast(F32)
@@ -128,10 +152,11 @@ def tile_structuredlstmcell_kernel(
                 b, bank = take_bank([P, 2, 2 * P])
                 for rg in range(2):
                     for u in range(2):
-                        col = (2 * half + rg) * (k_of[s] // 2) + first_word
-                        nc.tensor.transpose(
-                            bank[:, u, rg * P:(rg + 1) * P], words[:, col + u:col + CHUNK_WORDS:2], ident_f32[:]
-                        )
+                        if (j, c) in sorted_words:
+                            src_words = sorted_words[(j, c)][:, 2 * half + rg, u, :]
+                        else:
+                            src_words = words[:, 2 * half + rg, u:CHUNK_WORDS:2]
+                        nc.tensor.transpose(bank[:, u, rg * P:(rg + 1) * P], src_words, ident_f32[:])
                 banks.append((b, bank))
             for half in range(2):
                 b, bank = banks[half]
@@ -257,6 +282,8 @@ def tile_structuredlstmcell_kernel(
         transpose_chunk(0, 2, "ss")
         transpose_chunk(0, 3, "ss")
         load_block(RAW_BLOCKS)
+        sort_words(1, 0)
+        sort_words(1, 1)
         quantise(0, 2)
         quantise(0, 3)
         transpose_chunk(1, 0, "ss")
@@ -264,6 +291,8 @@ def tile_structuredlstmcell_kernel(
         for c in (2, 3):
             for t in range(N_TILES):
                 mx_pass(0, t, c)
+        sort_words(1, 2)
+        sort_words(1, 3)
         quantise(1, 0)
         quantise(1, 1)
         for t in range(N_TILES):
@@ -271,71 +300,111 @@ def tile_structuredlstmcell_kernel(
         transpose_chunk(1, 2, "ss")
         transpose_chunk(1, 3, "ss")
         load_block(RAW_BLOCKS + 1)
+        sigmoids(0, 0, 2)
+        tanh_candidate(0, 0, 2)
         quantise(1, 2)
         quantise(1, 3)
+        forget_times_cell(0, 0, 2)
+        input_times_candidate(0, 0, 2)
+        sum_to_cell(0, 0, 2)
 
-        for j in range(1, N_BLOCKS - 1):
+        def gate_functions(j, t0):
+            sigmoids(j, t0, t0 + 2)
+            tanh_candidate(j, t0, t0 + 2)
+
+        def cell_products(j, t0):
+            forget_times_cell(j, t0, t0 + 2)
+            input_times_candidate(j, t0, t0 + 2)
+            sum_to_cell(j, t0, t0 + 2)
+            if t0 == 2:
+                store(c_dram, c_new, j, 0, N_TILES)
+
+        def hidden_product(j, t0):
+            output_times_tanh(j, t0, t0 + 2)
+            if t0 == 2:
+                store(h_dram, h_new, j, 0, N_TILES)
+
+        for j in range(1, N_BLOCKS - 2):
             transpose_chunk(j + 1, 0, "ss")
             transpose_chunk(j + 1, 1, "ss")
+            sort_words(j + 1, 2)
             quantise(j + 1, 0)
             quantise(j + 1, 1)
-            sigmoids(j - 1, 0, N_TILES)
-            tanh_candidate(j - 1, 0, N_TILES)
+            tanh_cell(j - 1, 0, 2)
+            gate_functions(j - 1, 2)
             passes_and_bias(j, 0)
             passes_and_bias(j, 1)
-            forget_times_cell(j - 1, 0, N_TILES)
-            input_times_candidate(j - 1, 0, N_TILES)
-            sum_to_cell(j - 1, 0, N_TILES)
-            store(c_dram, c_new, j - 1, 0, N_TILES)
+            hidden_product(j - 1, 0)
+            cell_products(j - 1, 2)
             transpose_chunk(j + 1, 2, "ss")
             transpose_chunk(j + 1, 3, "ss")
             if j + 1 + RAW_BLOCKS < N_BLOCKS:
                 load_block(j + 1 + RAW_BLOCKS)
-            tanh_cell(j - 1, 0, N_TILES)
+            tanh_cell(j - 1, 2, 4)
+            gate_functions(j, 0)
+
             quantise(j + 1, 2)
             quantise(j + 1, 3)
             passes_and_bias(j, 2)
-            output_times_tanh(j - 1, 0, N_TILES)
-            store(h_dram, h_new, j - 1, 0, N_TILES)
+            hidden_product(j - 1, 2)
             passes_and_bias(j, 3)
+            cell_products(j, 0)
 
         last = N_BLOCKS - 1
         prev = last - 1
-        sigmoids(prev, 0, 2)
-        tanh_candidate(prev, 0, 2)
-        sigmoids(prev, 2, 4)
-        tanh_candidate(prev, 2, 4)
-        forget_times_cell(prev, 0, 2)
-        passes_and_bias(last, 0)
-        input_times_candidate(prev, 0, 2)
-        passes_and_bias(last, 1)
-        sum_to_cell(prev, 0, 2)
-        forget_times_cell(prev, 2, 4)
-        sigmoids(last, 0, 2)
+        transpose_chunk(last, 0, "ss")
+        transpose_chunk(last, 1, "ss")
+        quantise(last, 0)
+        quantise(last, 1)
+        tanh_cell(prev - 1, 0, 2)
+        gate_functions(prev - 1, 2)
+        passes_and_bias(prev, 0)
+        passes_and_bias(prev, 1)
+        hidden_product(prev - 1, 0)
+        cell_products(prev - 1, 2)
+        gate_functions(prev, 0)
+        tanh_cell(prev - 1, 2, 4)
+        passes_and_bias(prev, 2)
+        hidden_product(prev - 1, 2)
+        passes_and_bias(prev, 3)
+        transpose_chunk(last, 2, "ss")
+        transpose_chunk(last, 3, "ss")
+        cell_products(prev, 0)
+        quantise(last, 2)
         tanh_cell(prev, 0, 2)
-        tanh_candidate(last, 0, 2)
-        passes_and_bias(last, 2)
-        output_times_tanh(prev, 0, 2)
-        passes_and_bias(last, 3)
-        input_times_candidate(prev, 2, 4)
-        sum_to_cell(prev, 2, 4)
-        store(c_dram, c_new, prev, 0, N_TILES)
-        sigmoids(last, 2, 4)
+        gate_functions(prev, 2)
+        quantise(last, 3)
+        hidden_product(prev, 0)
+        for c in (0, 1):
+            for t in range(N_TILES):
+                mx_pass(last, t, c)
+        cell_products(prev, 2)
         tanh_cell(prev, 2, 4)
-        tanh_candidate(last, 2, 4)
-        forget_times_cell(last, 0, 2)
-        input_times_candidate(last, 0, 2)
-        output_times_tanh(prev, 2, 4)
-        store(h_dram, h_new, prev, 0, N_TILES)
-        sum_to_cell(last, 0, 2)
+        for t in range(N_TILES):
+            mx_pass(last, t, 2)
+            mx_pass(last, t, 3)
+        add_bias(last, 0)
+        sigmoids(last, 0, 1)
+        tanh_candidate(last, 0, 1)
+        add_bias(last, 1)
+        sigmoids(last, 1, 2)
+        tanh_candidate(last, 1, 2)
+        add_bias(last, 2)
+        sigmoids(last, 2, 3)
+        tanh_candidate(last, 2, 3)
+        add_bias(last, 3)
+        cell_products(last, 0)
         store(c_dram, c_new, last, 0, 2)
+        sigmoids(last, 3, 4)
+        tanh_candidate(last, 3, 4)
         tanh_cell(last, 0, 2)
+        hidden_product(prev, 2)
         forget_times_cell(last, 2, 4)
         input_times_candidate(last, 2, 4)
-        output_times_tanh(last, 0, 2)
-        store(h_dram, h_new, last, 0, 2)
         sum_to_cell(last, 2, 4)
         store(c_dram, c_new, last, 2, 4)
         tanh_cell(last, 2, 4)
+        hidden_product(last, 0)
+        store(h_dram, h_new, last, 0, 2)
         output_times_tanh(last, 2, 4)
         store(h_dram, h_new, last, 2, 4)

@@ -18,14 +18,15 @@ FLOPS = 2 * BATCH * K_TOTAL * 4 * HIDDEN
 
 P = 128
 N_TILES = BATCH // P
-N_BLOCKS = HIDDEN // P
+PAIR_COLS = 2 * P
+N_UNITS = 8
 N_CHUNKS = 4
 N_GATES = 4
-GATE_COLS = N_GATES * P
+BANK_COLS = 512
 CHUNK_WORDS = 256
 ACTS = -1
 WARM_UP_MATMULS = 4
-RAW_BLOCKS = 5
+RAW_UNITS = 5
 
 
 def tile_structuredlstmcell_kernel(
@@ -37,31 +38,30 @@ def tile_structuredlstmcell_kernel(
 ):
     nc = tc.nc
     weights = [
-        [W_pi, W_pf, W_po, W_pg],
-        [W_xi, W_xf, W_xo, W_xg],
-        [W_hi, W_hf, W_ho, W_hg],
+        [W_pi, W_pg, W_pf, W_po],
+        [W_xi, W_xg, W_xf, W_xo],
+        [W_hi, W_hg, W_hf, W_ho],
     ]
-    biases = [b_pi, b_pf, b_po, b_pg]
+    biases = [b_pi, b_pg, b_pf, b_po]
     activations = [p_in, ext_input, hidden]
     k_of = [512, 512, 1024]
-    col_i, col_f, col_o, col_g = [slice(g * P, (g + 1) * P) for g in range(N_GATES)]
+    first, second = slice(0, PAIR_COLS), slice(PAIR_COLS, BANK_COLS)
 
     with ExitStack() as ctx:
         ctx.enter_context(tc.manual_schedule())
         const = ctx.enter_context(tc.tile_pool(name="const", bufs=1))
-        raw_pool = ctx.enter_context(tc.tile_pool(name="raw", bufs=RAW_BLOCKS))
+        raw_pool = ctx.enter_context(tc.tile_pool(name="raw", bufs=RAW_UNITS))
         sorted_pool = ctx.enter_context(tc.tile_pool(name="sorted", bufs=4))
         grouped_pool = ctx.enter_context(tc.tile_pool(name="grouped", bufs=6))
         code_pool = ctx.enter_context(tc.tile_pool(name="codes", bufs=10))
-        gate_pool = ctx.enter_context(tc.tile_pool(name="gates", bufs=4))
-        out_pool = ctx.enter_context(tc.tile_pool(name="outs", bufs=3))
+        gate_pool = ctx.enter_context(tc.tile_pool(name="gates", bufs=2))
         psum = ctx.enter_context(tc.psum_pool(name="psum", bufs=1))
 
         ident_f32 = const.tile([P, P], F32, name="ident_f32")
         make_identity(nc, ident_f32[:])
-        bias_rows = const.tile([P, GATE_COLS], BF16, name="bias_rows")
+        bias_rows = const.tile([P, BANK_COLS], BF16, name="bias_rows")
         nc.vector.memset(bias_rows[:], 0.0)
-        zeros = const.tile([P, GATE_COLS], BF16, name="zeros")
+        zeros = const.tile([P, BANK_COLS], BF16, name="zeros")
         nc.vector.memset(zeros[:], 0.0)
         warm = const.tile([P, 1], F32, name="warm")
         nc.vector.memset(warm[:], 0.0)
@@ -88,24 +88,27 @@ def tile_structuredlstmcell_kernel(
                 nc.sync.dma_start(out=raw[(ACTS, s)][:, cols], in_=view[:, cols])
 
         def load_weights(j, s):
-            k = k_of[s]
-            raw[(j, s)] = raw_pool.tile([P, N_GATES * k], BF16, name="raw_w%d" % s, tag="raw_w%d" % s)
-            for g in range(N_GATES):
-                nc.sync.dma_start(out=raw[(j, s)][:, g * k:(g + 1) * k], in_=weights[s][g][j * P:(j + 1) * P, :])
+            run = 2 * k_of[s]
+            raw[(j, s)] = raw_pool.tile([P, 2 * run], BF16, name="raw_w%d" % s, tag="raw_w%d" % s)
+            rows = slice(j // 2 * PAIR_COLS, (j // 2 + 1) * PAIR_COLS)
+            for i in range(2):
+                view = weights[s][2 * (j % 2) + i][rows, :].rearrange("(p e) k -> p (e k)", e=2)
+                nc.sync.dma_start(out=raw[(j, s)][:, i * run:(i + 1) * run], in_=view)
 
-        def load_block(j):
+        def load_unit(j):
             for s in range(3):
                 load_weights(j, s)
 
         for s in range(3):
             load_activation(s)
             load_weights(0, s)
-        load_block(1)
+        load_unit(1)
+        load_unit(2)
         nc.sync.dma_start(
             out=cell_sb[:].rearrange("p t h -> p (t h)"), in_=cell.rearrange("(p t) h -> p (t h)", t=N_TILES)
         )
-        for j in range(2, RAW_BLOCKS):
-            load_block(j)
+        for j in range(3, RAW_UNITS):
+            load_unit(j)
 
         free_banks = list(range(8))
 
@@ -113,19 +116,16 @@ def tile_structuredlstmcell_kernel(
             b = free_banks.pop(0)
             return b, psum.tile(shape, F32, name="bank%d" % b, tag="bank%d" % b)
 
-        b_warm, warm_bank = take_bank([P, GATE_COLS])
+        b_warm, warm_bank = take_bank([P, BANK_COLS])
         for i in range(WARM_UP_MATMULS):
             nc.tensor.matmul(out=warm_bank[:], lhsT=zeros[:, 0:P], rhs=zeros[:], start=True, stop=True)
         free_banks.append(b_warm)
 
+        sorted_words = {}
         grouped = {}
         w_codes = {}
         acc = {}
         gates = {}
-        c_new = {}
-        h_new = {}
-
-        sorted_words = {}
 
         def chunk_words(j, c):
             s = min(c, 2)
@@ -133,35 +133,34 @@ def tile_structuredlstmcell_kernel(
             words = raw[(j, s)][:].bitcast(F32).rearrange("p (r w) -> p r w", r=4)
             return words[:, :, first_word:first_word + CHUNK_WORDS]
 
-        def sort_words(j, c, engine="v"):
-            tile = sorted_pool.tile([P, 4, 2, P], F32, name="sorted_words", tag="sorted_words")
-            src = chunk_words(j, c).rearrange("p r (w u) -> p r u w", u=2)
-            if engine == "v":
-                nc.vector.tensor_copy(out=tile[:], in_=src)
-            else:
-                nc.scalar.copy(out=tile[:], in_=src)
-            sorted_words[(j, c)] = tile
+        def sort_words(j, c):
+            if j < N_UNITS:
+                tile = sorted_pool.tile([P, 4, 2, P], F32, name="sorted_words", tag="sorted_words")
+                nc.vector.tensor_copy(out=tile[:], in_=chunk_words(j, c).rearrange("p r (w u) -> p r u w", u=2))
+                sorted_words[(j, c)] = tile
 
         def transpose_chunk(j, c, engines):
-            words = chunk_words(j, c)
-            out_tile = grouped_pool.tile([P, 4 * GATE_COLS], BF16, name="grouped", tag="grouped", align_bytes=64)
+            out_tile = grouped_pool.tile([P, 4 * BANK_COLS], BF16, name="grouped", tag="grouped", align_bytes=64)
             grouped[(j, c)] = out_tile
             out_words = out_tile[:].bitcast(F32)
             banks = []
             for half in range(2):
-                b, bank = take_bank([P, 2, 2 * P])
-                for rg in range(2):
+                b, bank = take_bank([P, 2, 2, P])
+                for e in range(2):
                     for u in range(2):
                         if (j, c) in sorted_words:
-                            src_words = sorted_words[(j, c)][:, 2 * half + rg, u, :]
+                            words = sorted_words[(j, c)][:, 2 * half + e, u, :]
                         else:
-                            src_words = words[:, 2 * half + rg, u:CHUNK_WORDS:2]
-                        nc.tensor.transpose(bank[:, u, rg * P:(rg + 1) * P], src_words, ident_f32[:])
+                            words = chunk_words(j, c)[:, 2 * half + e, u:CHUNK_WORDS:2]
+                        nc.tensor.transpose(bank[:, u, e, :], words, ident_f32[:])
                 banks.append((b, bank))
             for half in range(2):
                 b, bank = banks[half]
-                dst = out_words[:, half * GATE_COLS:(half + 1) * GATE_COLS].rearrange("p (n u) -> p n u", u=2)
-                src = bank[:].rearrange("p u n -> p n u")
+                dst = out_words[:, half * BANK_COLS:(half + 1) * BANK_COLS]
+                if j == ACTS:
+                    dst, src = dst.rearrange("p (e n u) -> p e n u", e=2, u=2), bank[:].rearrange("p u e n -> p e n u")
+                else:
+                    dst, src = dst.rearrange("p (n e u) -> p n e u", e=2, u=2), bank[:].rearrange("p u e n -> p n e u")
                 if engines[half] == "s":
                     nc.scalar.copy(out=dst, in_=src)
                 else:
@@ -172,15 +171,15 @@ def tile_structuredlstmcell_kernel(
             if j == ACTS:
                 codes, scales = act_codes[:, c, :], act_scales[:, c, :]
             else:
-                codes_tile = code_pool.tile([P, GATE_COLS], U32, name="w_codes", tag="w_codes", align_bytes=64)
-                scales_tile = code_pool.tile([P, GATE_COLS], U8, name="w_scales", tag="w_scales", align_bytes=64)
+                codes_tile = code_pool.tile([P, BANK_COLS], U32, name="w_codes", tag="w_codes", align_bytes=64)
+                scales_tile = code_pool.tile([P, BANK_COLS], U8, name="w_scales", tag="w_scales", align_bytes=64)
                 w_codes[(j, c)] = (codes_tile, scales_tile)
                 codes, scales = codes_tile[:], scales_tile[:]
             nc.vector.quantize_mx(out=codes.bitcast(FP8X4), scales=scales, in_=grouped[(j, c)][:])
 
         def mx_pass(j, t, c):
             if c == 0:
-                acc[(j, t)] = take_bank([P, GATE_COLS])
+                acc[(j, t)] = take_bank([P, BANK_COLS])
             codes_tile, scales_tile = w_codes[(j, c)]
             rows = slice(t * P, (t + 1) * P)
             nc.tensor.matmul_mx(
@@ -195,25 +194,30 @@ def tile_structuredlstmcell_kernel(
 
         def spread_bias(first_row):
             for r in range(first_row, first_row + 4):
-                b, bank = take_bank([P, GATE_COLS])
+                b, bank = take_bank([P, BANK_COLS])
                 nc.tensor.matmul(
                     out=bank[:], lhsT=ident_bf16[:, r:r + 1].to_broadcast([P, P]), rhs=bias_rows[:], start=True, stop=True
                 )
-                dst = bias_all[:, r // 2, (r % 2) * GATE_COLS:(r % 2 + 1) * GATE_COLS]
+                dst = bias_all[:, r // 2, (r % 2) * BANK_COLS:(r % 2 + 1) * BANK_COLS]
                 if r % 2 == 0:
                     nc.scalar.copy(out=dst, in_=bank[:])
                 else:
                     nc.vector.tensor_copy(out=dst, in_=bank[:])
                 free_banks.append(b)
 
+        def pair_cols(j):
+            return slice(j // 2 * PAIR_COLS, (j // 2 + 1) * PAIR_COLS)
+
         def add_bias(j, t):
             if t == 0:
-                gates[j] = gate_pool.tile([P, N_TILES, GATE_COLS], F32, name="gates", tag="gates")
+                tag = "gates_fo" if j % 2 else "gates_ig"
+                gates[j] = gate_pool.tile([P, N_TILES, BANK_COLS], F32, name=tag, tag=tag)
             b, bank = acc[(j, t)]
+            g = 2 * (j % 2)
             nc.vector.tensor_tensor(
-                out=gates[j][:, t, :].rearrange("p (g n) -> p g n", g=N_GATES),
-                in0=bank[:].rearrange("p (g n) -> p g n", g=N_GATES),
-                in1=bias_all[:, :, j * P:(j + 1) * P],
+                out=gates[j][:, t, :].rearrange("p (g n) -> p g n", g=2),
+                in0=bank[:].rearrange("p (g n) -> p g n", g=2),
+                in1=bias_all[:, g:g + 2, pair_cols(j)],
                 op=ALU.add,
             )
             free_banks.append(b)
@@ -223,44 +227,37 @@ def tile_structuredlstmcell_kernel(
                 mx_pass(j, t, c)
             add_bias(j, t)
 
-        def sigmoids(j, t0, t1):
-            v = gates[j][:, t0:t1, 0:3 * P]
-            nc.scalar.activation(out=v, in_=v, func=ACT.Sigmoid)
+        def function(j, cols, func, t0, t1):
+            v = gates[j][:, t0:t1, cols]
+            nc.scalar.activation(out=v, in_=v, func=func)
 
-        def tanh_candidate(j, t0, t1):
-            v = gates[j][:, t0:t1, col_g]
-            nc.scalar.activation(out=v, in_=v, func=ACT.Tanh)
-
-        def forget_times_cell(j, t0, t1):
-            v = gates[j][:, t0:t1, col_f]
-            nc.vector.tensor_tensor(out=v, in0=v, in1=cell_sb[:, t0:t1, j * P:(j + 1) * P], op=ALU.mult)
+        def gate_functions(j, t0, t1):
+            function(j, first, ACT.Sigmoid, t0, t1)
+            function(j, second, ACT.Sigmoid if j % 2 else ACT.Tanh, t0, t1)
 
         def input_times_candidate(j, t0, t1):
-            v = gates[j][:, t0:t1, col_i]
-            nc.vector.tensor_tensor(out=v, in0=v, in1=gates[j][:, t0:t1, col_g], op=ALU.mult)
+            v = gates[j][:, t0:t1, first]
+            nc.vector.tensor_tensor(out=v, in0=v, in1=gates[j][:, t0:t1, second], op=ALU.mult)
+
+        def forget_times_cell(j, t0, t1):
+            v = gates[j][:, t0:t1, first]
+            nc.vector.tensor_tensor(out=v, in0=v, in1=cell_sb[:, t0:t1, pair_cols(j)], op=ALU.mult)
 
         def sum_to_cell(j, t0, t1):
-            if j not in c_new:
-                c_new[j] = out_pool.tile([P, N_TILES, P], F32, name="c_new", tag="c_new")
-            nc.vector.tensor_tensor(
-                out=c_new[j][:, t0:t1, :], in0=gates[j][:, t0:t1, col_f], in1=gates[j][:, t0:t1, col_i], op=ALU.add
-            )
+            v = gates[j][:, t0:t1, first]
+            nc.vector.tensor_tensor(out=v, in0=v, in1=gates[j - 1][:, t0:t1, first], op=ALU.add)
+            nc.sync.dma_start(out=c_dram[:, t0:t1, pair_cols(j)], in_=v)
 
         def tanh_cell(j, t0, t1):
-            nc.scalar.activation(out=gates[j][:, t0:t1, col_g], in_=c_new[j][:, t0:t1, :], func=ACT.Tanh)
+            nc.scalar.activation(out=gates[j - 1][:, t0:t1, second], in_=gates[j][:, t0:t1, first], func=ACT.Tanh)
 
         def output_times_tanh(j, t0, t1):
-            if j not in h_new:
-                h_new[j] = out_pool.tile([P, N_TILES, P], F32, name="h_new", tag="h_new")
-            nc.vector.tensor_tensor(
-                out=h_new[j][:, t0:t1, :], in0=gates[j][:, t0:t1, col_o], in1=gates[j][:, t0:t1, col_g], op=ALU.mult
-            )
+            v = gates[j][:, t0:t1, second]
+            nc.vector.tensor_tensor(out=v, in0=v, in1=gates[j - 1][:, t0:t1, second], op=ALU.mult)
+            nc.sync.dma_start(out=h_dram[:, t0:t1, pair_cols(j)], in_=v)
 
         h_dram = out_0.rearrange("(p t) h -> p t h", t=N_TILES)
         c_dram = out_1.rearrange("(p t) h -> p t h", t=N_TILES)
-
-        def store(dram, tiles, j, t0, t1):
-            nc.sync.dma_start(out=dram[:, t0:t1, j * P:(j + 1) * P], in_=tiles[j][:, t0:t1, :])
 
         transpose_chunk(ACTS, 0, "sv")
         spread_bias(0)
@@ -281,7 +278,7 @@ def tile_structuredlstmcell_kernel(
         quantise(ACTS, 3)
         transpose_chunk(0, 2, "ss")
         transpose_chunk(0, 3, "ss")
-        load_block(RAW_BLOCKS)
+        load_unit(RAW_UNITS)
         sort_words(1, 0)
         sort_words(1, 1)
         quantise(0, 2)
@@ -299,112 +296,64 @@ def tile_structuredlstmcell_kernel(
             add_bias(0, t)
         transpose_chunk(1, 2, "ss")
         transpose_chunk(1, 3, "ss")
-        load_block(RAW_BLOCKS + 1)
-        sigmoids(0, 0, 2)
-        tanh_candidate(0, 0, 2)
+        load_unit(RAW_UNITS + 1)
         quantise(1, 2)
         quantise(1, 3)
-        forget_times_cell(0, 0, 2)
-        input_times_candidate(0, 0, 2)
-        sum_to_cell(0, 0, 2)
 
-        def gate_functions(j, t0):
-            sigmoids(j, t0, t0 + 2)
-            tanh_candidate(j, t0, t0 + 2)
-
-        def cell_products(j, t0):
-            forget_times_cell(j, t0, t0 + 2)
-            input_times_candidate(j, t0, t0 + 2)
-            sum_to_cell(j, t0, t0 + 2)
-            if t0 == 2:
-                store(c_dram, c_new, j, 0, N_TILES)
-
-        def hidden_product(j, t0):
-            output_times_tanh(j, t0, t0 + 2)
-            if t0 == 2:
-                store(h_dram, h_new, j, 0, N_TILES)
-
-        for j in range(1, N_BLOCKS - 2):
+        for j in range(1, N_UNITS - 1):
             transpose_chunk(j + 1, 0, "ss")
             transpose_chunk(j + 1, 1, "ss")
-            sort_words(j + 1, 2)
+            gate_functions(j - 1, 0, N_TILES)
+            if j % 2:
+                sort_words(j + 1, 2)
             quantise(j + 1, 0)
+            if j % 2:
+                sort_words(j + 1, 3)
             quantise(j + 1, 1)
-            tanh_cell(j - 1, 0, 2)
-            gate_functions(j - 1, 2)
             passes_and_bias(j, 0)
             passes_and_bias(j, 1)
-            hidden_product(j - 1, 0)
-            cell_products(j - 1, 2)
+            if j % 2:
+                input_times_candidate(j - 1, 0, N_TILES)
+                sort_words(j + 2, 0)
+                sort_words(j + 2, 1)
+            else:
+                forget_times_cell(j - 1, 0, N_TILES)
+                sum_to_cell(j - 1, 0, N_TILES)
             transpose_chunk(j + 1, 2, "ss")
             transpose_chunk(j + 1, 3, "ss")
-            if j + 1 + RAW_BLOCKS < N_BLOCKS:
-                load_block(j + 1 + RAW_BLOCKS)
-            tanh_cell(j - 1, 2, 4)
-            gate_functions(j, 0)
-
+            if j + 1 + RAW_UNITS < N_UNITS:
+                load_unit(j + 1 + RAW_UNITS)
+            if j % 2 == 0:
+                tanh_cell(j - 1, 0, N_TILES)
             quantise(j + 1, 2)
             quantise(j + 1, 3)
             passes_and_bias(j, 2)
-            hidden_product(j - 1, 2)
+            if j % 2 == 0:
+                output_times_tanh(j - 1, 0, N_TILES)
             passes_and_bias(j, 3)
-            cell_products(j, 0)
 
-        last = N_BLOCKS - 1
-        prev = last - 1
-        transpose_chunk(last, 0, "ss")
-        transpose_chunk(last, 1, "ss")
-        quantise(last, 0)
-        quantise(last, 1)
-        tanh_cell(prev - 1, 0, 2)
-        gate_functions(prev - 1, 2)
-        passes_and_bias(prev, 0)
-        passes_and_bias(prev, 1)
-        hidden_product(prev - 1, 0)
-        cell_products(prev - 1, 2)
-        gate_functions(prev, 0)
-        tanh_cell(prev - 1, 2, 4)
-        passes_and_bias(prev, 2)
-        hidden_product(prev - 1, 2)
-        passes_and_bias(prev, 3)
-        transpose_chunk(last, 2, "ss")
-        transpose_chunk(last, 3, "ss")
-        cell_products(prev, 0)
-        quantise(last, 2)
-        tanh_cell(prev, 0, 2)
-        gate_functions(prev, 2)
-        quantise(last, 3)
-        hidden_product(prev, 0)
-        for c in (0, 1):
-            for t in range(N_TILES):
-                mx_pass(last, t, c)
-        cell_products(prev, 2)
-        tanh_cell(prev, 2, 4)
-        for t in range(N_TILES):
-            mx_pass(last, t, 2)
-            mx_pass(last, t, 3)
-        add_bias(last, 0)
-        sigmoids(last, 0, 1)
-        tanh_candidate(last, 0, 1)
-        add_bias(last, 1)
-        sigmoids(last, 1, 2)
-        tanh_candidate(last, 1, 2)
-        add_bias(last, 2)
-        sigmoids(last, 2, 3)
-        tanh_candidate(last, 2, 3)
-        add_bias(last, 3)
-        cell_products(last, 0)
-        store(c_dram, c_new, last, 0, 2)
-        sigmoids(last, 3, 4)
-        tanh_candidate(last, 3, 4)
+        last = N_UNITS - 1
+        halves = ((0, 2), (2, N_TILES))
+        gate_functions(last - 1, 0, 2)
+        gate_functions(last - 1, 2, N_TILES)
+        passes_and_bias(last, 0)
+        input_times_candidate(last - 1, 0, 2)
+        passes_and_bias(last, 1)
+        input_times_candidate(last - 1, 2, N_TILES)
+        gate_functions(last, 0, 2)
+        forget_times_cell(last, 0, 2)
+        sum_to_cell(last, 0, 2)
+        passes_and_bias(last, 2)
         tanh_cell(last, 0, 2)
-        hidden_product(prev, 2)
-        forget_times_cell(last, 2, 4)
-        input_times_candidate(last, 2, 4)
-        sum_to_cell(last, 2, 4)
-        store(c_dram, c_new, last, 2, 4)
-        tanh_cell(last, 2, 4)
-        hidden_product(last, 0)
-        store(h_dram, h_new, last, 0, 2)
-        output_times_tanh(last, 2, 4)
-        store(h_dram, h_new, last, 2, 4)
+        gate_functions(last, 2, 3)
+        passes_and_bias(last, 3)
+        output_times_tanh(last, 0, 2)
+        forget_times_cell(last, 2, 3)
+        sum_to_cell(last, 2, 3)
+        gate_functions(last, 3, 4)
+        tanh_cell(last, 2, 3)
+        forget_times_cell(last, 3, 4)
+        sum_to_cell(last, 3, 4)
+        tanh_cell(last, 3, 4)
+        output_times_tanh(last, 2, 3)
+        output_times_tanh(last, 3, 4)

@@ -61,18 +61,24 @@ def tile_structuredlstmcell_kernel(
         make_identity(nc, ident_f32[:])
         bias_rows = const.tile([P, BANK_COLS], BF16, name="bias_rows")
         nc.vector.memset(bias_rows[:], 0.0)
+        bias_blocks = const.tile([P, P], BF16, name="bias_blocks")
+        nc.vector.memset(bias_blocks[:], 0.0)
         zeros = const.tile([P, BANK_COLS], BF16, name="zeros")
         nc.vector.memset(zeros[:], 0.0)
         warm = const.tile([P, 1], F32, name="warm")
         nc.vector.memset(warm[:], 0.0)
-        for g in range(N_GATES):
+        for i in range(2):
             nc.scalar.dma_start(
-                out=bias_rows[2 * g:2 * g + 2, :], in_=biases[g].rearrange("(r n) -> r n", r=2)
+                out=bias_rows[2 * i:2 * i + 2, :], in_=biases[2 + i].rearrange("(r n) -> r n", r=2)
+            )
+            nc.scalar.dma_start(
+                out=bias_blocks[8 * i:8 * i + 8, :], in_=biases[i].rearrange("(r n) -> r n", r=8)
             )
         nc.scalar.activation(out=warm[:], in_=warm[:], func=ACT.Sigmoid)
         ident_bf16 = const.tile([P, P], BF16, name="ident_bf16")
         nc.vector.tensor_copy(out=ident_bf16[:], in_=ident_f32[:])
-        bias_all = const.tile([P, N_GATES, HIDDEN], BF16, name="bias_all")
+        bias_all = const.tile([P, 2, HIDDEN], BF16, name="bias_all")
+        bias_cols = const.tile([P, 2, HIDDEN // P], F32, name="bias_cols")
         cell_sb = const.tile([P, N_TILES, HIDDEN], BF16, name="cell_sb")
         act_codes = const.tile([P, N_CHUNKS, BATCH], U32, name="act_codes", align_bytes=64)
         act_scales = const.tile([P, N_CHUNKS, BATCH], U8, name="act_scales", align_bytes=64)
@@ -126,6 +132,7 @@ def tile_structuredlstmcell_kernel(
         w_codes = {}
         acc = {}
         gates = {}
+        turned = {}
 
         def chunk_words(j, c):
             s = min(c, 2)
@@ -177,83 +184,112 @@ def tile_structuredlstmcell_kernel(
                 codes, scales = codes_tile[:], scales_tile[:]
             nc.vector.quantize_mx(out=codes.bitcast(FP8X4), scales=scales, in_=grouped[(j, c)][:])
 
-        def mx_pass(j, t, c):
+        def mx_pass(j, m, c):
             if c == 0:
-                acc[(j, t)] = take_bank([P, BANK_COLS])
+                acc[(j, m)] = take_bank([P, BANK_COLS])
             codes_tile, scales_tile = w_codes[(j, c)]
-            rows = slice(t * P, (t + 1) * P)
+            cols = slice(m * P, (m + 1) * P)
+            activation = (act_codes[:, c, :], act_scales[:, c, :])
+            weight = (codes_tile[:], scales_tile[:])
+            stationary, moving = (activation, weight) if j % 2 else (weight, activation)
             nc.tensor.matmul_mx(
-                out=acc[(j, t)][1][:],
-                lhsT=act_codes[:, c, rows].bitcast(FP8X4),
-                lhsT_scale=act_scales[:, c, rows],
-                rhs=codes_tile[:].bitcast(FP8X4),
-                rhs_scale=scales_tile[:],
+                out=acc[(j, m)][1][:],
+                lhsT=stationary[0][:, cols].bitcast(FP8X4),
+                lhsT_scale=stationary[1][:, cols],
+                rhs=moving[0].bitcast(FP8X4),
+                rhs_scale=moving[1],
                 start=(c == 0),
                 stop=(c == N_CHUNKS - 1),
             )
 
-        def spread_bias(first_row):
-            for r in range(first_row, first_row + 4):
-                b, bank = take_bank([P, BANK_COLS])
-                nc.tensor.matmul(
-                    out=bank[:], lhsT=ident_bf16[:, r:r + 1].to_broadcast([P, P]), rhs=bias_rows[:], start=True, stop=True
-                )
-                dst = bias_all[:, r // 2, (r % 2) * BANK_COLS:(r % 2 + 1) * BANK_COLS]
-                if r % 2 == 0:
-                    nc.scalar.copy(out=dst, in_=bank[:])
-                else:
-                    nc.vector.tensor_copy(out=dst, in_=bank[:])
-                free_banks.append(b)
+        def passes(j, m):
+            for c in range(N_CHUNKS):
+                mx_pass(j, m, c)
+
+        def spread_bias(r):
+            b, bank = take_bank([P, BANK_COLS])
+            nc.tensor.matmul(
+                out=bank[:], lhsT=ident_bf16[:, r:r + 1].to_broadcast([P, P]), rhs=bias_rows[:], start=True, stop=True
+            )
+            dst = bias_all[:, r // 2, (r % 2) * BANK_COLS:(r % 2 + 1) * BANK_COLS]
+            if r % 2 == 0:
+                nc.scalar.copy(out=dst, in_=bank[:])
+            else:
+                nc.vector.tensor_copy(out=dst, in_=bank[:])
+            free_banks.append(b)
+
+        def turn_bias():
+            b = free_banks.pop(0)
+            bank = psum.tile([P, P], BF16, name="bank%d" % b, tag="bank%d" % b)
+            nc.tensor.transpose(bank[:], bias_blocks[:], ident_bf16[:])
+            nc.vector.tensor_copy(out=bias_cols[:].rearrange("p g r -> p (g r)"), in_=bank[:, 0:16])
+            free_banks.append(b)
 
         def pair_cols(j):
             return slice(j // 2 * PAIR_COLS, (j // 2 + 1) * PAIR_COLS)
 
+        def gate_function(j, m):
+            if m == 0:
+                gates[j] = gate_pool.tile([P, 2, 2, BATCH], F32, name="gates_ig", tag="gates_ig")
+            g, half = divmod(m, 2)
+            b, bank = acc[(j, m)]
+            col = 2 * (j // 2) + half
+            nc.scalar.activation(
+                out=gates[j][:, g, half, :], in_=bank[:], func=ACT.Tanh if g else ACT.Sigmoid,
+                bias=bias_cols[:, g, col:col + 1],
+            )
+            free_banks.append(b)
+
+        def input_times_candidate(j, half):
+            v = gates[j][:, 0, half, :]
+            nc.vector.tensor_tensor(out=v, in0=v, in1=gates[j][:, 1, half, :], op=ALU.mult)
+
+        def turn_input(j):
+            for half in range(2):
+                turned[(j, half)] = take_bank([P, N_TILES, P])
+                for t in range(N_TILES):
+                    nc.tensor.transpose(
+                        turned[(j, half)][1][:, t, :], gates[j][:, 0, half, t * P:(t + 1) * P], ident_f32[:]
+                    )
+
         def add_bias(j, t):
             if t == 0:
-                tag = "gates_fo" if j % 2 else "gates_ig"
-                gates[j] = gate_pool.tile([P, N_TILES, BANK_COLS], F32, name=tag, tag=tag)
+                gates[j] = gate_pool.tile([P, N_TILES, BANK_COLS], F32, name="gates_fo", tag="gates_fo")
             b, bank = acc[(j, t)]
-            g = 2 * (j % 2)
             nc.vector.tensor_tensor(
                 out=gates[j][:, t, :].rearrange("p (g n) -> p g n", g=2),
                 in0=bank[:].rearrange("p (g n) -> p g n", g=2),
-                in1=bias_all[:, g:g + 2, pair_cols(j)],
+                in1=bias_all[:, :, pair_cols(j)],
                 op=ALU.add,
             )
             free_banks.append(b)
 
-        def passes_and_bias(j, t):
-            for c in range(N_CHUNKS):
-                mx_pass(j, t, c)
-            add_bias(j, t)
-
-        def function(j, cols, func, t0, t1):
-            v = gates[j][:, t0:t1, cols]
-            nc.scalar.activation(out=v, in_=v, func=func)
-
-        def gate_functions(j, t0, t1):
-            function(j, first, ACT.Sigmoid, t0, t1)
-            function(j, second, ACT.Sigmoid if j % 2 else ACT.Tanh, t0, t1)
-
-        def input_times_candidate(j, t0, t1):
-            v = gates[j][:, t0:t1, first]
-            nc.vector.tensor_tensor(out=v, in0=v, in1=gates[j][:, t0:t1, second], op=ALU.mult)
+        def sigmoids(j, t0, t1):
+            v = gates[j][:, t0:t1, :]
+            nc.scalar.activation(out=v, in_=v, func=ACT.Sigmoid)
 
         def forget_times_cell(j, t0, t1):
             v = gates[j][:, t0:t1, first]
             nc.vector.tensor_tensor(out=v, in0=v, in1=cell_sb[:, t0:t1, pair_cols(j)], op=ALU.mult)
 
         def sum_to_cell(j, t0, t1):
-            v = gates[j][:, t0:t1, first]
-            nc.vector.tensor_tensor(out=v, in0=v, in1=gates[j - 1][:, t0:t1, first], op=ALU.add)
-            nc.sync.dma_start(out=c_dram[:, t0:t1, pair_cols(j)], in_=v)
+            for half in range(2):
+                b, bank = turned[(j - 1, half)]
+                v = gates[j][:, t0:t1, half * P:(half + 1) * P]
+                nc.vector.tensor_tensor(out=v, in0=bank[:, t0:t1, :], in1=v, op=ALU.add)
+                if t1 == N_TILES:
+                    free_banks.append(b)
+            nc.sync.dma_start(out=c_dram[:, t0:t1, pair_cols(j)], in_=gates[j][:, t0:t1, first])
+
+        def tanh_of_cell(j):
+            return gates[j - 1][:, 1, :, :].rearrange("p s b -> p (s b)").rearrange("p (t n) -> p t n", t=N_TILES)
 
         def tanh_cell(j, t0, t1):
-            nc.scalar.activation(out=gates[j - 1][:, t0:t1, second], in_=gates[j][:, t0:t1, first], func=ACT.Tanh)
+            nc.scalar.activation(out=tanh_of_cell(j)[:, t0:t1, :], in_=gates[j][:, t0:t1, first], func=ACT.Tanh)
 
         def output_times_tanh(j, t0, t1):
             v = gates[j][:, t0:t1, second]
-            nc.vector.tensor_tensor(out=v, in0=v, in1=gates[j - 1][:, t0:t1, second], op=ALU.mult)
+            nc.vector.tensor_tensor(out=v, in0=v, in1=tanh_of_cell(j)[:, t0:t1, :], op=ALU.mult)
             nc.sync.dma_start(out=h_dram[:, t0:t1, pair_cols(j)], in_=v)
 
         h_dram = out_0.rearrange("(p t) h -> p t h", t=N_TILES)
@@ -261,19 +297,25 @@ def tile_structuredlstmcell_kernel(
 
         transpose_chunk(ACTS, 0, "sv")
         spread_bias(0)
+        spread_bias(1)
         transpose_chunk(0, 0, "sv")
         quantise(ACTS, 0)
         transpose_chunk(ACTS, 1, "sv")
         quantise(0, 0)
-        spread_bias(4)
+        spread_bias(2)
+        spread_bias(3)
+        turn_bias()
         transpose_chunk(0, 1, "sv")
         quantise(ACTS, 1)
+        for m in range(4):
+            mx_pass(0, m, 0)
         transpose_chunk(ACTS, 2, "ss")
         quantise(0, 1)
         transpose_chunk(ACTS, 3, "ss")
-        for c in (0, 1):
-            for t in range(N_TILES):
-                mx_pass(0, t, c)
+        for m in range(4):
+            mx_pass(0, m, 1)
+        sort_words(0, 2)
+        sort_words(0, 3)
         quantise(ACTS, 2)
         quantise(ACTS, 3)
         transpose_chunk(0, 2, "ss")
@@ -286,71 +328,96 @@ def tile_structuredlstmcell_kernel(
         transpose_chunk(1, 0, "ss")
         transpose_chunk(1, 1, "ss")
         for c in (2, 3):
-            for t in range(N_TILES):
-                mx_pass(0, t, c)
+            for m in range(4):
+                mx_pass(0, m, c)
         sort_words(1, 2)
         sort_words(1, 3)
         quantise(1, 0)
         quantise(1, 1)
-        for t in range(N_TILES):
-            add_bias(0, t)
+        gate_function(0, 0)
+        gate_function(0, 2)
         transpose_chunk(1, 2, "ss")
         transpose_chunk(1, 3, "ss")
         load_unit(RAW_UNITS + 1)
+        sort_words(2, 1)
         quantise(1, 2)
         quantise(1, 3)
 
         for j in range(1, N_UNITS - 1):
             transpose_chunk(j + 1, 0, "ss")
             transpose_chunk(j + 1, 1, "ss")
-            gate_functions(j - 1, 0, N_TILES)
-            if j % 2:
-                sort_words(j + 1, 2)
+            sort_words(j + 1, 2)
             quantise(j + 1, 0)
-            if j % 2:
-                sort_words(j + 1, 3)
+            sort_words(j + 1, 3)
             quantise(j + 1, 1)
-            passes_and_bias(j, 0)
-            passes_and_bias(j, 1)
             if j % 2:
-                input_times_candidate(j - 1, 0, N_TILES)
-                sort_words(j + 2, 0)
-                sort_words(j + 2, 1)
+                gate_function(j - 1, 1)
+                gate_function(j - 1, 3)
+                passes(j, 0)
+                add_bias(j, 0)
+                passes(j, 1)
+                add_bias(j, 1)
+                input_times_candidate(j - 1, 0)
+                input_times_candidate(j - 1, 1)
             else:
+                sigmoids(j - 1, 2, N_TILES)
+                passes(j, 0)
+                passes(j, 2)
                 forget_times_cell(j - 1, 0, N_TILES)
-                sum_to_cell(j - 1, 0, N_TILES)
+                gate_function(j, 0)
+                gate_function(j, 2)
             transpose_chunk(j + 1, 2, "ss")
             transpose_chunk(j + 1, 3, "ss")
             if j + 1 + RAW_UNITS < N_UNITS:
                 load_unit(j + 1 + RAW_UNITS)
+            if j % 2:
+                sigmoids(j, 0, 2)
+                sort_words(j + 2, 0)
+                sort_words(j + 2, 1)
+            else:
+                turn_input(j - 2)
+                sort_words(j + 2, 1)
             if j % 2 == 0:
+                sum_to_cell(j - 1, 0, N_TILES)
                 tanh_cell(j - 1, 0, N_TILES)
             quantise(j + 1, 2)
             quantise(j + 1, 3)
-            passes_and_bias(j, 2)
-            if j % 2 == 0:
+            if j % 2:
+                passes(j, 2)
+                add_bias(j, 2)
+                passes(j, 3)
+                add_bias(j, 3)
+            else:
+                passes(j, 1)
+                passes(j, 3)
+
                 output_times_tanh(j - 1, 0, N_TILES)
-            passes_and_bias(j, 3)
 
         last = N_UNITS - 1
-        halves = ((0, 2), (2, N_TILES))
-        gate_functions(last - 1, 0, 2)
-        gate_functions(last - 1, 2, N_TILES)
-        passes_and_bias(last, 0)
-        input_times_candidate(last - 1, 0, 2)
-        passes_and_bias(last, 1)
-        input_times_candidate(last - 1, 2, N_TILES)
-        gate_functions(last, 0, 2)
-        forget_times_cell(last, 0, 2)
+        gate_function(last - 1, 1)
+        gate_function(last - 1, 3)
+        input_times_candidate(last - 1, 0)
+        passes(last, 0)
+        add_bias(last, 0)
+        input_times_candidate(last - 1, 1)
+        sigmoids(last, 0, 1)
+        passes(last, 1)
+        add_bias(last, 1)
+        sigmoids(last, 1, 2)
+        passes(last, 2)
+        turn_input(last - 1)
+        forget_times_cell(last, 0, 1)
+        add_bias(last, 2)
+        sigmoids(last, 2, 3)
+        forget_times_cell(last, 1, 2)
+        passes(last, 3)
         sum_to_cell(last, 0, 2)
-        passes_and_bias(last, 2)
+        add_bias(last, 3)
         tanh_cell(last, 0, 2)
-        gate_functions(last, 2, 3)
-        passes_and_bias(last, 3)
-        output_times_tanh(last, 0, 2)
+        sigmoids(last, 3, 4)
         forget_times_cell(last, 2, 3)
+        output_times_tanh(last, 0, 2)
         sum_to_cell(last, 2, 3)
-        gate_functions(last, 3, 4)
         tanh_cell(last, 2, 3)
         forget_times_cell(last, 3, 4)
         sum_to_cell(last, 3, 4)

@@ -242,7 +242,8 @@ def tile_structuredlstmcell_kernel(
 
         def input_times_candidate(j, half):
             v = gates[j][:, 0, half, :]
-            nc.vector.tensor_tensor(out=v, in0=v, in1=gates[j][:, 1, half, :], op=ALU.mult)
+            engine = nc.gpsimd if j < N_UNITS - 2 else nc.vector
+            engine.tensor_tensor(out=v, in0=v, in1=gates[j][:, 1, half, :], op=ALU.mult)
 
         def turn_input(j):
             for half in range(2):
@@ -314,13 +315,13 @@ def tile_structuredlstmcell_kernel(
         transpose_chunk(ACTS, 3, "ss")
         for m in range(4):
             mx_pass(0, m, 1)
+        quantise(ACTS, 2)
         sort_words(0, 2)
         sort_words(0, 3)
-        quantise(ACTS, 2)
-        quantise(ACTS, 3)
         transpose_chunk(0, 2, "ss")
         transpose_chunk(0, 3, "ss")
         load_unit(RAW_UNITS)
+        quantise(ACTS, 3)
         sort_words(1, 0)
         sort_words(1, 1)
         quantise(0, 2)
@@ -376,10 +377,10 @@ def tile_structuredlstmcell_kernel(
                 sort_words(j + 2, 1)
             else:
                 turn_input(j - 2)
-                sort_words(j + 2, 1)
-            if j % 2 == 0:
                 sum_to_cell(j - 1, 0, N_TILES)
                 tanh_cell(j - 1, 0, N_TILES)
+                sort_words(j + 2, 0)
+                sort_words(j + 2, 1)
             quantise(j + 1, 2)
             quantise(j + 1, 3)
             if j % 2:

@@ -242,8 +242,7 @@ def tile_structuredlstmcell_kernel(
 
         def input_times_candidate(j, half):
             v = gates[j][:, 0, half, :]
-            engine = nc.gpsimd if j < N_UNITS - 2 else nc.vector
-            engine.tensor_tensor(out=v, in0=v, in1=gates[j][:, 1, half, :], op=ALU.mult)
+            nc.gpsimd.tensor_tensor(out=v, in0=v, in1=gates[j][:, 1, half, :], op=ALU.mult)
 
         def turn_input(j):
             for half in range(2):
@@ -394,34 +393,61 @@ def tile_structuredlstmcell_kernel(
 
                 output_times_tanh(j - 1, 0, N_TILES)
 
+        def gate_passes(j, t, g):
+            acc[(j, t, g)] = take_bank([P, PAIR_COLS])
+            rows, cols = slice(t * P, (t + 1) * P), slice(g * PAIR_COLS, (g + 1) * PAIR_COLS)
+            for c in range(N_CHUNKS):
+                codes_tile, scales_tile = w_codes[(j, c)]
+                nc.tensor.matmul_mx(
+                    out=acc[(j, t, g)][1][:],
+                    lhsT=act_codes[:, c, rows].bitcast(FP8X4),
+                    lhsT_scale=act_scales[:, c, rows],
+                    rhs=codes_tile[:, cols].bitcast(FP8X4),
+                    rhs_scale=scales_tile[:, cols],
+                    start=(c == 0),
+                    stop=(c == N_CHUNKS - 1),
+                )
+
+        def add_gate_bias(j, t, g):
+            if t == 0 and g == 0:
+                gates[j] = gate_pool.tile([P, N_TILES, BANK_COLS], F32, name="gates_fo", tag="gates_fo")
+            b, bank = acc[(j, t, g)]
+            nc.vector.tensor_tensor(
+                out=gates[j][:, t, g * PAIR_COLS:(g + 1) * PAIR_COLS], in0=bank[:], in1=bias_all[:, g, pair_cols(j)], op=ALU.add
+            )
+            free_banks.append(b)
+
+        def gate_sigmoid(j, t0, t1, g):
+            v = gates[j][:, t0:t1, g * PAIR_COLS:(g + 1) * PAIR_COLS]
+            nc.scalar.activation(out=v, in_=v, func=ACT.Sigmoid)
+
         last = N_UNITS - 1
         gate_function(last - 1, 1)
         gate_function(last - 1, 3)
         input_times_candidate(last - 1, 0)
-        passes(last, 0)
-        add_bias(last, 0)
         input_times_candidate(last - 1, 1)
-        sigmoids(last, 0, 1)
-        passes(last, 1)
-        add_bias(last, 1)
-        sigmoids(last, 1, 2)
-        passes(last, 2)
+        for t in range(N_TILES):
+            gate_passes(last, t, 0)
+            add_gate_bias(last, t, 0)
+        gate_sigmoid(last, 0, 2, 0)
+        gate_sigmoid(last, 2, 4, 0)
+        gate_passes(last, 0, 1)
+        gate_passes(last, 1, 1)
         turn_input(last - 1)
-        forget_times_cell(last, 0, 1)
-        add_bias(last, 2)
-        sigmoids(last, 2, 3)
-        forget_times_cell(last, 1, 2)
-        passes(last, 3)
+        gate_passes(last, 2, 1)
+        gate_passes(last, 3, 1)
+        forget_times_cell(last, 0, 2)
+        forget_times_cell(last, 2, 4)
         sum_to_cell(last, 0, 2)
-        add_bias(last, 3)
+        add_gate_bias(last, 0, 1)
+        add_gate_bias(last, 1, 1)
         tanh_cell(last, 0, 2)
-        sigmoids(last, 3, 4)
-        forget_times_cell(last, 2, 3)
+        gate_sigmoid(last, 0, 2, 1)
+        sum_to_cell(last, 2, 4)
+        tanh_cell(last, 2, 4)
+        add_gate_bias(last, 2, 1)
+        add_gate_bias(last, 3, 1)
+        gate_sigmoid(last, 2, 4, 1)
         output_times_tanh(last, 0, 2)
-        sum_to_cell(last, 2, 3)
-        tanh_cell(last, 2, 3)
-        forget_times_cell(last, 3, 4)
-        sum_to_cell(last, 3, 4)
-        tanh_cell(last, 3, 4)
         output_times_tanh(last, 2, 3)
         output_times_tanh(last, 3, 4)

@@ -25,7 +25,7 @@ N_GATES = 4
 BANK_COLS = 512
 CHUNK_WORDS = 256
 ACTS = -1
-WARM_UP_MATMULS = 4
+WARM_UP_MATMULS = 16
 RAW_UNITS = 5
 
 
@@ -57,23 +57,16 @@ def tile_structuredlstmcell_kernel(
         gate_pool = ctx.enter_context(tc.tile_pool(name="gates", bufs=2))
         psum = ctx.enter_context(tc.psum_pool(name="psum", bufs=1))
 
+        zeros = const.tile([P, P], BF16, name="zeros")
+        nc.vector.memset(zeros[:], 0.0)
         ident_f32 = const.tile([P, P], F32, name="ident_f32")
         make_identity(nc, ident_f32[:])
         bias_rows = const.tile([P, BANK_COLS], BF16, name="bias_rows")
         nc.vector.memset(bias_rows[:], 0.0)
         bias_blocks = const.tile([P, P], BF16, name="bias_blocks")
         nc.vector.memset(bias_blocks[:], 0.0)
-        zeros = const.tile([P, BANK_COLS], BF16, name="zeros")
-        nc.vector.memset(zeros[:], 0.0)
         warm = const.tile([P, 1], F32, name="warm")
         nc.vector.memset(warm[:], 0.0)
-        for i in range(2):
-            nc.scalar.dma_start(
-                out=bias_rows[2 * i:2 * i + 2, :], in_=biases[2 + i].rearrange("(r n) -> r n", r=2)
-            )
-            nc.scalar.dma_start(
-                out=bias_blocks[8 * i:8 * i + 8, :], in_=biases[i].rearrange("(r n) -> r n", r=8)
-            )
         nc.scalar.activation(out=warm[:], in_=warm[:], func=ACT.Sigmoid)
         ident_bf16 = const.tile([P, P], BF16, name="ident_bf16")
         nc.vector.tensor_copy(out=ident_bf16[:], in_=ident_f32[:])
@@ -108,6 +101,15 @@ def tile_structuredlstmcell_kernel(
         for s in range(3):
             load_activation(s)
             load_weights(0, s)
+            if s == 1:
+                for i in range(2):
+                    nc.sync.dma_start(
+                        out=bias_rows[2 * i:2 * i + 2, :], in_=biases[2 + i].rearrange("(r n) -> r n", r=2)
+                    )
+        for i in range(2):
+            nc.sync.dma_start(
+                out=bias_blocks[8 * i:8 * i + 8, :], in_=biases[i].rearrange("(r n) -> r n", r=8)
+            )
         load_unit(1)
         load_unit(2)
         nc.sync.dma_start(
@@ -122,9 +124,9 @@ def tile_structuredlstmcell_kernel(
             b = free_banks.pop(0)
             return b, psum.tile(shape, F32, name="bank%d" % b, tag="bank%d" % b)
 
-        b_warm, warm_bank = take_bank([P, BANK_COLS])
+        b_warm, warm_bank = take_bank([P, P])
         for i in range(WARM_UP_MATMULS):
-            nc.tensor.matmul(out=warm_bank[:], lhsT=zeros[:, 0:P], rhs=zeros[:], start=True, stop=True)
+            nc.tensor.matmul(out=warm_bank[:], lhsT=zeros[:], rhs=zeros[:], start=True, stop=True)
         free_banks.append(b_warm)
 
         sorted_words = {}
@@ -296,17 +298,14 @@ def tile_structuredlstmcell_kernel(
         c_dram = out_1.rearrange("(p t) h -> p t h", t=N_TILES)
 
         transpose_chunk(ACTS, 0, "sv")
-        spread_bias(0)
-        spread_bias(1)
         transpose_chunk(0, 0, "sv")
         quantise(ACTS, 0)
         transpose_chunk(ACTS, 1, "sv")
         quantise(0, 0)
-        spread_bias(2)
-        spread_bias(3)
-        turn_bias()
         transpose_chunk(0, 1, "sv")
         quantise(ACTS, 1)
+        for r in range(4):
+            spread_bias(r)
         for m in range(4):
             mx_pass(0, m, 0)
         transpose_chunk(ACTS, 2, "ss")
@@ -314,9 +313,10 @@ def tile_structuredlstmcell_kernel(
         transpose_chunk(ACTS, 3, "ss")
         for m in range(4):
             mx_pass(0, m, 1)
-        quantise(ACTS, 2)
         sort_words(0, 2)
+        quantise(ACTS, 2)
         sort_words(0, 3)
+        turn_bias()
         transpose_chunk(0, 2, "ss")
         transpose_chunk(0, 3, "ss")
         load_unit(RAW_UNITS)

from contextlib import ExitStack

import concourse.mybir as mybir
from concourse.masks import make_identity

F32 = mybir.dt.float32
BF16 = mybir.dt.bfloat16
U32 = mybir.dt.uint32
U8 = mybir.dt.uint8
FP8X4 = mybir.dt.float8_e4m3fn_x4
ACT = mybir.ActivationFunctionType
ALU = mybir.AluOpType

BATCH = 512
HIDDEN = 1024
K_TOTAL = 2048
FLOPS = 2 * BATCH * K_TOTAL * 4 * HIDDEN

P = 128
N_TILES = BATCH // P
PAIR_COLS = 2 * P
N_UNITS = 8
N_CHUNKS = 4
N_GATES = 4
BANK_COLS = 512
CHUNK_WORDS = 256
ACTS = -1
WARM_UP_MATMULS = 16
RAW_UNITS = 5


def tile_structuredlstmcell_kernel(
    tc, p_in, hidden, cell, ext_input,
    W_pi, b_pi, W_pf, b_pf, W_pg, b_pg, W_po, b_po,
    W_hi, W_hf, W_hg, W_ho,
    W_xi, W_xf, W_xg, W_xo,
    out_0, out_1,
):
    nc = tc.nc
    weights = [
        [W_pi, W_pg, W_pf, W_po],
        [W_xi, W_xg, W_xf, W_xo],
        [W_hi, W_hg, W_hf, W_ho],
    ]
    biases = [b_pi, b_pg, b_pf, b_po]
    activations = [p_in, ext_input, hidden]
    k_of = [512, 512, 1024]
    first, second = slice(0, PAIR_COLS), slice(PAIR_COLS, BANK_COLS)

    with ExitStack() as ctx:
        ctx.enter_context(tc.manual_schedule())
        const = ctx.enter_context(tc.tile_pool(name="const", bufs=1))
        raw_pool = ctx.enter_context(tc.tile_pool(name="raw", bufs=RAW_UNITS))
        sorted_pool = ctx.enter_context(tc.tile_pool(name="sorted", bufs=4))
        grouped_pool = ctx.enter_context(tc.tile_pool(name="grouped", bufs=6))
        code_pool = ctx.enter_context(tc.tile_pool(name="codes", bufs=10))
        gate_pool = ctx.enter_context(tc.tile_pool(name="gates", bufs=2))
        psum = ctx.enter_context(tc.psum_pool(name="psum", bufs=1))

        zeros = const.tile([P, P], BF16, name="zeros")
        nc.vector.memset(zeros[:], 0.0)
        ident_f32 = const.tile([P, P], F32, name="ident_f32")
        make_identity(nc, ident_f32[:])
        bias_rows = const.tile([P, BANK_COLS], BF16, name="bias_rows")
        nc.vector.memset(bias_rows[:], 0.0)
        bias_blocks = const.tile([P, P], BF16, name="bias_blocks")
        nc.vector.memset(bias_blocks[:], 0.0)
        warm = const.tile([P, 1], F32, name="warm")
        nc.vector.memset(warm[:], 0.0)
        nc.scalar.activation(out=warm[:], in_=warm[:], func=ACT.Sigmoid)
        ident_bf16 = const.tile([P, P], BF16, name="ident_bf16")
        nc.vector.tensor_copy(out=ident_bf16[:], in_=ident_f32[:])
        bias_all = const.tile([P, 2, HIDDEN], BF16, name="bias_all")
        bias_cols = const.tile([P, 2, HIDDEN // P], F32, name="bias_cols")
        cell_sb = const.tile([P, N_TILES, HIDDEN], BF16, name="cell_sb")
        act_codes = const.tile([P, N_CHUNKS, BATCH], U32, name="act_codes", align_bytes=64)
        act_scales = const.tile([P, N_CHUNKS, BATCH], U8, name="act_scales", align_bytes=64)

        raw = {}

        def load_activation(s):
            raw[(ACTS, s)] = const.tile([P, N_TILES * k_of[s]], BF16, name="raw_act%d" % s)
            view = activations[s].rearrange("(p t) k -> p (t k)", t=N_TILES)
            half_cols = 2 * k_of[s]
            for part in range(2):
                cols = slice(part * half_cols, (part + 1) * half_cols)
                nc.sync.dma_start(out=raw[(ACTS, s)][:, cols], in_=view[:, cols])

        def load_weights(j, s):
            run = 2 * k_of[s]
            raw[(j, s)] = raw_pool.tile([P, 2 * run], BF16, name="raw_w%d" % s, tag="raw_w%d" % s)
            rows = slice(j // 2 * PAIR_COLS, (j // 2 + 1) * PAIR_COLS)
            for i in range(2):
                view = weights[s][2 * (j % 2) + i][rows, :].rearrange("(p e) k -> p (e k)", e=2)
                nc.sync.dma_start(out=raw[(j, s)][:, i * run:(i + 1) * run], in_=view)

        def load_unit(j):
            for s in range(3):
                load_weights(j, s)

        for s in range(3):
            load_activation(s)
            load_weights(0, s)
            if s == 1:
                for i in range(2):
                    nc.sync.dma_start(
                        out=bias_rows[2 * i:2 * i + 2, :], in_=biases[2 + i].rearrange("(r n) -> r n", r=2)
                    )
        for i in range(2):
            nc.sync.dma_start(
                out=bias_blocks[8 * i:8 * i + 8, :], in_=biases[i].rearrange("(r n) -> r n", r=8)
            )
        load_unit(1)
        load_unit(2)
        nc.sync.dma_start(
            out=cell_sb[:].rearrange("p t h -> p (t h)"), in_=cell.rearrange("(p t) h -> p (t h)", t=N_TILES)
        )
        for j in range(3, RAW_UNITS):
            load_unit(j)

        free_banks = list(range(8))

        def take_bank(shape):
            b = free_banks.pop(0)
            return b, psum.tile(shape, F32, name="bank%d" % b, tag="bank%d" % b)

        b_warm, warm_bank = take_bank([P, P])
        for i in range(WARM_UP_MATMULS):
            nc.tensor.matmul(out=warm_bank[:], lhsT=zeros[:], rhs=zeros[:], start=True, stop=True)
        free_banks.append(b_warm)

        sorted_words = {}
        grouped = {}
        w_codes = {}
        acc = {}
        gates = {}
        turned = {}

        def chunk_words(j, c):
            s = min(c, 2)
            first_word = CHUNK_WORDS * (c - 2) if c > 2 else 0
            words = raw[(j, s)][:].bitcast(F32).rearrange("p (r w) -> p r w", r=4)
            return words[:, :, first_word:first_word + CHUNK_WORDS]

        def sort_words(j, c):
            if j < N_UNITS:
                tile = sorted_pool.tile([P, 4, 2, P], F32, name="sorted_words", tag="sorted_words")
                nc.vector.tensor_copy(out=tile[:], in_=chunk_words(j, c).rearrange("p r (w u) -> p r u w", u=2))
                sorted_words[(j, c)] = tile

        def transpose_chunk(j, c, engines):
            out_tile = grouped_pool.tile([P, 4 * BANK_COLS], BF16, name="grouped", tag="grouped", align_bytes=64)
            grouped[(j, c)] = out_tile
            out_words = out_tile[:].bitcast(F32)
            banks = []
            for half in range(2):
                b, bank = take_bank([P, 2, 2, P])
                for e in range(2):
                    for u in range(2):
                        if (j, c) in sorted_words:
                            words = sorted_words[(j, c)][:, 2 * half + e, u, :]
                        else:
                            words = chunk_words(j, c)[:, 2 * half + e, u:CHUNK_WORDS:2]
                        nc.tensor.transpose(bank[:, u, e, :], words, ident_f32[:])
                banks.append((b, bank))
            for half in range(2):
                b, bank = banks[half]
                dst = out_words[:, half * BANK_COLS:(half + 1) * BANK_COLS]
                if j == ACTS:
                    dst, src = dst.rearrange("p (e n u) -> p e n u", e=2, u=2), bank[:].rearrange("p u e n -> p e n u")
                else:
                    dst, src = dst.rearrange("p (n e u) -> p n e u", e=2, u=2), bank[:].rearrange("p u e n -> p n e u")
                if engines[half] == "s":
                    nc.scalar.copy(out=dst, in_=src)
                else:
                    nc.vector.tensor_copy(out=dst, in_=src)
                free_banks.append(b)

        def quantise(j, c):
            if j == ACTS:
                codes, scales = act_codes[:, c, :], act_scales[:, c, :]
            else:
                codes_tile = code_pool.tile([P, BANK_COLS], U32, name="w_codes", tag="w_codes", align_bytes=64)
                scales_tile = code_pool.tile([P, BANK_COLS], U8, name="w_scales", tag="w_scales", align_bytes=64)
                w_codes[(j, c)] = (codes_tile, scales_tile)
                codes, scales = codes_tile[:], scales_tile[:]
            nc.vector.quantize_mx(out=codes.bitcast(FP8X4), scales=scales, in_=grouped[(j, c)][:])

        def mx_pass(j, m, c):
            if c == 0:
                acc[(j, m)] = take_bank([P, BANK_COLS])
            codes_tile, scales_tile = w_codes[(j, c)]
            cols = slice(m * P, (m + 1) * P)
            activation = (act_codes[:, c, :], act_scales[:, c, :])
            weight = (codes_tile[:], scales_tile[:])
            stationary, moving = (activation, weight) if j % 2 else (weight, activation)
            nc.tensor.matmul_mx(
                out=acc[(j, m)][1][:],
                lhsT=stationary[0][:, cols].bitcast(FP8X4),
                lhsT_scale=stationary[1][:, cols],
                rhs=moving[0].bitcast(FP8X4),
                rhs_scale=moving[1],
                start=(c == 0),
                stop=(c == N_CHUNKS - 1),
            )

        def passes(j, m):
            for c in range(N_CHUNKS):
                mx_pass(j, m, c)

        def spread_bias(r):
            b, bank = take_bank([P, BANK_COLS])
            nc.tensor.matmul(
                out=bank[:], lhsT=ident_bf16[:, r:r + 1].to_broadcast([P, P]), rhs=bias_rows[:], start=True, stop=True
            )
            dst = bias_all[:, r // 2, (r % 2) * BANK_COLS:(r % 2 + 1) * BANK_COLS]
            if r % 2 == 0:
                nc.scalar.copy(out=dst, in_=bank[:])
            else:
                nc.vector.tensor_copy(out=dst, in_=bank[:])
            free_banks.append(b)

        def turn_bias():
            b = free_banks.pop(0)
            bank = psum.tile([P, P], BF16, name="bank%d" % b, tag="bank%d" % b)
            nc.tensor.transpose(bank[:], bias_blocks[:], ident_bf16[:])
            nc.vector.tensor_copy(out=bias_cols[:].rearrange("p g r -> p (g r)"), in_=bank[:, 0:16])
            free_banks.append(b)

        def pair_cols(j):
            return slice(j // 2 * PAIR_COLS, (j // 2 + 1) * PAIR_COLS)

        def gate_function(j, m):
            if m == 0:
                gates[j] = gate_pool.tile([P, 2, 2, BATCH], F32, name="gates_ig", tag="gates_ig")
            g, half = divmod(m, 2)
            b, bank = acc[(j, m)]
            col = 2 * (j // 2) + half
            nc.scalar.activation(
                out=gates[j][:, g, half, :], in_=bank[:], func=ACT.Tanh if g else ACT.Sigmoid,
                bias=bias_cols[:, g, col:col + 1],
            )
            free_banks.append(b)

        def input_times_candidate(j, half):
            v = gates[j][:, 0, half, :]
            nc.gpsimd.tensor_tensor(out=v, in0=v, in1=gates[j][:, 1, half, :], op=ALU.mult)

        def turn_input(j):
            for half in range(2):
                turned[(j, half)] = take_bank([P, N_TILES, P])
                for t in range(N_TILES):
                    nc.tensor.transpose(
                        turned[(j, half)][1][:, t, :], gates[j][:, 0, half, t * P:(t + 1) * P], ident_f32[:]
                    )

        def add_bias(j, t):
            if t == 0:
                gates[j] = gate_pool.tile([P, N_TILES, BANK_COLS], F32, name="gates_fo", tag="gates_fo")
            b, bank = acc[(j, t)]
            nc.vector.tensor_tensor(
                out=gates[j][:, t, :].rearrange("p (g n) -> p g n", g=2),
                in0=bank[:].rearrange("p (g n) -> p g n", g=2),
                in1=bias_all[:, :, pair_cols(j)],
                op=ALU.add,
            )
            free_banks.append(b)

        def sigmoids(j, t0, t1):
            v = gates[j][:, t0:t1, :]
            nc.scalar.activation(out=v, in_=v, func=ACT.Sigmoid)

        def forget_times_cell(j, t0, t1):
            v = gates[j][:, t0:t1, first]
            nc.vector.tensor_tensor(out=v, in0=v, in1=cell_sb[:, t0:t1, pair_cols(j)], op=ALU.mult)

        def sum_to_cell(j, t0, t1):
            for half in range(2):
                b, bank = turned[(j - 1, half)]
                v = gates[j][:, t0:t1, half * P:(half + 1) * P]
                nc.vector.tensor_tensor(out=v, in0=bank[:, t0:t1, :], in1=v, op=ALU.add)
                if t1 == N_TILES:
                    free_banks.append(b)
            nc.sync.dma_start(out=c_dram[:, t0:t1, pair_cols(j)], in_=gates[j][:, t0:t1, first])

        def tanh_of_cell(j):
            return gates[j - 1][:, 1, :, :].rearrange("p s b -> p (s b)").rearrange("p (t n) -> p t n", t=N_TILES)

        def tanh_cell(j, t0, t1):
            nc.scalar.activation(out=tanh_of_cell(j)[:, t0:t1, :], in_=gates[j][:, t0:t1, first], func=ACT.Tanh)

        def output_times_tanh(j, t0, t1):
            v = gates[j][:, t0:t1, second]
            nc.vector.tensor_tensor(out=v, in0=v, in1=tanh_of_cell(j)[:, t0:t1, :], op=ALU.mult)
            nc.sync.dma_start(out=h_dram[:, t0:t1, pair_cols(j)], in_=v)

        h_dram = out_0.rearrange("(p t) h -> p t h", t=N_TILES)
        c_dram = out_1.rearrange("(p t) h -> p t h", t=N_TILES)

        transpose_chunk(ACTS, 0, "sv")
        transpose_chunk(0, 0, "sv")
        quantise(ACTS, 0)
        transpose_chunk(ACTS, 1, "sv")
        quantise(0, 0)
        transpose_chunk(0, 1, "sv")
        quantise(ACTS, 1)
        for r in range(4):
            spread_bias(r)
        for m in range(4):
            mx_pass(0, m, 0)
        transpose_chunk(ACTS, 2, "ss")
        quantise(0, 1)
        transpose_chunk(ACTS, 3, "ss")
        for m in range(4):
            mx_pass(0, m, 1)
        sort_words(0, 2)
        quantise(ACTS, 2)
        sort_words(0, 3)
        turn_bias()
        transpose_chunk(0, 2, "ss")
        transpose_chunk(0, 3, "ss")
        load_unit(RAW_UNITS)
        quantise(ACTS, 3)
        sort_words(1, 0)
        sort_words(1, 1)
        quantise(0, 2)
        quantise(0, 3)
        transpose_chunk(1, 0, "ss")
        transpose_chunk(1, 1, "ss")
        for c in (2, 3):
            for m in range(4):
                mx_pass(0, m, c)
        sort_words(1, 2)
        sort_words(1, 3)
        quantise(1, 0)
        quantise(1, 1)
        gate_function(0, 0)
        gate_function(0, 2)
        transpose_chunk(1, 2, "ss")
        transpose_chunk(1, 3, "ss")
        load_unit(RAW_UNITS + 1)
        sort_words(2, 1)
        quantise(1, 2)
        quantise(1, 3)

        for j in range(1, N_UNITS - 1):
            transpose_chunk(j + 1, 0, "ss")
            transpose_chunk(j + 1, 1, "ss")
            sort_words(j + 1, 2)
            quantise(j + 1, 0)
            sort_words(j + 1, 3)
            quantise(j + 1, 1)
            if j % 2:
                gate_function(j - 1, 1)
                gate_function(j - 1, 3)
                passes(j, 0)
                add_bias(j, 0)
                passes(j, 1)
                add_bias(j, 1)
                input_times_candidate(j - 1, 0)
                input_times_candidate(j - 1, 1)
            else:
                sigmoids(j - 1, 2, N_TILES)
                passes(j, 0)
                passes(j, 2)
                forget_times_cell(j - 1, 0, N_TILES)
                gate_function(j, 0)
                gate_function(j, 2)
            transpose_chunk(j + 1, 2, "ss")
            transpose_chunk(j + 1, 3, "ss")
            if j + 1 + RAW_UNITS < N_UNITS:
                load_unit(j + 1 + RAW_UNITS)
            if j % 2:
                sigmoids(j, 0, 2)
                sort_words(j + 2, 0)
                sort_words(j + 2, 1)
            else:
                turn_input(j - 2)
                sum_to_cell(j - 1, 0, N_TILES)
                tanh_cell(j - 1, 0, N_TILES)
                sort_words(j + 2, 0)
                sort_words(j + 2, 1)
            quantise(j + 1, 2)
            quantise(j + 1, 3)
            if j % 2:
                passes(j, 2)
                add_bias(j, 2)
                passes(j, 3)
                add_bias(j, 3)
            else:
                passes(j, 1)
                passes(j, 3)

                output_times_tanh(j - 1, 0, N_TILES)

        def gate_passes(j, t, g):
            acc[(j, t, g)] = take_bank([P, PAIR_COLS])
            rows, cols = slice(t * P, (t + 1) * P), slice(g * PAIR_COLS, (g + 1) * PAIR_COLS)
            for c in range(N_CHUNKS):
                codes_tile, scales_tile = w_codes[(j, c)]
                nc.tensor.matmul_mx(
                    out=acc[(j, t, g)][1][:],
                    lhsT=act_codes[:, c, rows].bitcast(FP8X4),
                    lhsT_scale=act_scales[:, c, rows],
                    rhs=codes_tile[:, cols].bitcast(FP8X4),
                    rhs_scale=scales_tile[:, cols],
                    start=(c == 0),
                    stop=(c == N_CHUNKS - 1),
                )

        def add_gate_bias(j, t, g):
            if t == 0 and g == 0:
                gates[j] = gate_pool.tile([P, N_TILES, BANK_COLS], F32, name="gates_fo", tag="gates_fo")
            b, bank = acc[(j, t, g)]
            nc.vector.tensor_tensor(
                out=gates[j][:, t, g * PAIR_COLS:(g + 1) * PAIR_COLS], in0=bank[:], in1=bias_all[:, g, pair_cols(j)], op=ALU.add
            )
            free_banks.append(b)

        def gate_sigmoid(j, t0, t1, g):
            v = gates[j][:, t0:t1, g * PAIR_COLS:(g + 1) * PAIR_COLS]
            nc.scalar.activation(out=v, in_=v, func=ACT.Sigmoid)

        last = N_UNITS - 1
        gate_function(last - 1, 1)
        gate_function(last - 1, 3)
        input_times_candidate(last - 1, 0)
        input_times_candidate(last - 1, 1)
        for t in range(N_TILES):
            gate_passes(last, t, 0)
            add_gate_bias(last, t, 0)
        gate_sigmoid(last, 0, 2, 0)
        gate_sigmoid(last, 2, 4, 0)
        gate_passes(last, 0, 1)
        gate_passes(last, 1, 1)
        turn_input(last - 1)
        gate_passes(last, 2, 1)
        gate_passes(last, 3, 1)
        forget_times_cell(last, 0, 2)
        forget_times_cell(last, 2, 4)
        sum_to_cell(last, 0, 2)
        add_gate_bias(last, 0, 1)
        add_gate_bias(last, 1, 1)
        tanh_cell(last, 0, 2)
        gate_sigmoid(last, 0, 2, 1)
        sum_to_cell(last, 2, 4)
        tanh_cell(last, 2, 4)
        add_gate_bias(last, 2, 1)
        add_gate_bias(last, 3, 1)
        gate_sigmoid(last, 2, 4, 1)
        output_times_tanh(last, 0, 2)
        output_times_tanh(last, 2, 3)
        output_times_tanh(last, 3, 4)
